import numpy as np
import ml_dtypes


def mxq(x, axis, fmt="e4m3"):
    dtype, down = {"e4m3": (ml_dtypes.float8_e4m3fn, 7), "e5m2": (ml_dtypes.float8_e5m2, 14)}[fmt]
    v = np.moveaxis(np.asarray(x, np.float32).astype(ml_dtypes.bfloat16).astype(np.float64), axis, -1)
    blocks = v.reshape(v.shape[:-1] + (-1, 32))
    amax = np.abs(blocks).max(-1, keepdims=True)
    byte = np.maximum(np.where(amax > 0, np.frexp(amax)[1] - 1 + 127, 0) - down, 1)
    scale = np.exp2(byte - 127.0)
    codes = (blocks / scale).astype(np.float32).astype(dtype).astype(np.float64)
    return np.moveaxis((codes * scale).reshape(v.shape), -1, axis)


WIDE = False


def mx_kscale(k):
    if not WIDE:
        return np.ones(k)
    levels = np.array([10, -10, 5, -5, 0])
    a = np.random.permutation(np.resize(levels, k // 512 * 4)).reshape(k // 512, 4)
    idx = np.arange(k)
    return np.exp2(a[idx // 512, idx % 128 // 32])


BF16 = ml_dtypes.bfloat16


def bf(x):
    return np.asarray(x, np.float32).astype(BF16)


def f64(x):
    return np.asarray(x).astype(np.float64)


E2M1 = np.array([0.0, 0.5, 1.0, 1.5, 2.0, 3.0, 4.0, 6.0, -0.0, -0.5, -1.0, -1.5, -2.0, -3.0, -4.0, -6.0])


def pack_weight(w, fmt):
    k, n = w.shape
    w = f64(bf(w)).reshape(k // 32, 32, n)
    amax = np.abs(w).max(1)
    if fmt == "e4m3":
        byte = np.frexp(amax)[1] - 1 + 127 - 7
    else:
        mant, ex = np.frexp(amax / 6.0)
        byte = np.where(mant > 0.5, ex, ex - 1) + 127
    byte = np.clip(np.where(amax > 0, byte, 1), 1, 254)
    scaled = (w * np.exp2(127.0 - byte)[:, None, :]).reshape(k, n).astype(np.float32)
    by_word = np.ascontiguousarray(scaled.reshape(k // 512, 128, 4, n).transpose(0, 1, 3, 2))
    if fmt == "e4m3":
        words = by_word.astype(ml_dtypes.float8_e4m3fn).view(np.uint8)
    else:
        c = by_word.astype(ml_dtypes.float4_e2m1fn).view(np.uint8) & 0xF
        words = c[..., 0::2] | (c[..., 1::2] << 4)
    return np.ascontiguousarray(words), np.ascontiguousarray(byte.astype(np.uint8).reshape(k // 512, 16, n))


def unpack_weight(words, scales, fmt):
    g, p, n, _ = words.shape
    if fmt == "e4m3":
        vals = np.ascontiguousarray(words).view(ml_dtypes.float8_e4m3fn).astype(np.float64)
    else:
        nib = np.empty((g, p, n, 4), np.uint8)
        nib[..., 0::2] = words & 0xF
        nib[..., 1::2] = words >> 4
        vals = E2M1[nib]
    vals = vals * np.repeat(np.exp2(scales.astype(np.float64) - 127.0), 8, axis=1)[..., None]
    return vals.transpose(0, 1, 3, 2).reshape(g * 512, n)

def pack4(w):
    words, scales = pack_weight(w, "e2m1")
    return words.reshape(words.shape[0], 128, -1), scales


def unpack4(words, scales):
    return unpack_weight(words.reshape(words.shape[0], 128, -1, 2), scales, "e2m1")


B, S, D, F, P, NQ = 2, 128, 1024, 1024, 1024, 3
LN_EPS = 1e-5


def layernorm(v, g, b):
    m = v.mean(-1, keepdims=True)
    var = v.var(-1, keepdims=True)
    return (v - m) / np.sqrt(var + LN_EPS) * g + b


def setup_inputs():
    s = mx_kscale(P)
    in_proto = bf(np.random.standard_normal((NQ, F, P)) * s)
    pt_w = np.random.standard_normal((NQ, D, P)) / np.sqrt(P) / s
    cat = np.ascontiguousarray(pt_w.swapaxes(1, 2)).reshape(-1, D)
    words, scales = pack4(cat)
    return {"in_proto": in_proto,
            "pt_w_words": words,
            "pt_w_scales": scales,
            "pln_g": bf(1.0 + 0.1 * np.random.standard_normal((NQ, D))),
            "pln_b": bf(0.1 * np.random.standard_normal((NQ, D))),
            "proto_w": bf(np.random.standard_normal((NQ, F, D)) * 0.5)}


def reference(in_proto, pt_w_words, pt_w_scales, pln_g, pln_b, proto_w):
    prc = mxq(f64(in_proto), 2, "e4m3") @ unpack4(pt_w_words, pt_w_scales).reshape(NQ, P, D)
    return f64(proto_w) + layernorm(prc, f64(pln_g)[:, None, :], f64(pln_b)[:, None, :])

@@ -1,0 +1,222 @@
+import concourse.mybir as mybir
+from concourse.masks import make_identity
+
+F32 = mybir.dt.float32
+BF16 = mybir.dt.bfloat16
+I32 = mybir.dt.int32
+U32 = mybir.dt.uint32
+U8 = mybir.dt.uint8
+FP8X4 = mybir.dt.float8_e4m3fn_x4
+FP4X4 = mybir.dt.float4_e2m1fn_x4
+ALU = mybir.AluOpType
+ACT = mybir.ActivationFunctionType
+
+BANKS = 3
+ROWS = 1024
+K = 1024
+D = 1024
+LN_EPS = 1e-5
+
+P = 128
+K_PASS = 4 * P
+PASSES = K // K_PASS
+HALF = 512
+HALVES = D // HALF
+ROW_TILES = ROWS // P
+PAIR = 2
+CHUNKS_PER_BANK = ROW_TILES // PAIR
+CHUNKS = BANKS * CHUNKS_PER_BANK
+LOADS_AHEAD = 3
+
+FLOPS = 2 * BANKS * ROWS * K * D
+
+
+def tile_moietransformerblock_pb_e_kernel(
+    tc, in_proto, pt_w_words, pt_w_scales, pln_g, pln_b, proto_w, out
+):
+    nc = tc.nc
+
+    x_rows = in_proto.rearrange("n (p t) k -> n p t k", t=ROW_TILES)
+    pw_rows = proto_w.rearrange("n (p t) d -> n p t d", t=ROW_TILES)
+    out_rows = out.rearrange("n (p t) d -> n p t d", t=ROW_TILES)
+
+    with (
+        tc.tile_pool(name="consts", bufs=1) as consts,
+        tc.tile_pool(name="x_pool", bufs=LOADS_AHEAD + 1) as x_pool,
+        tc.tile_pool(name="pw_pool", bufs=LOADS_AHEAD + 1) as pw_pool,
+        tc.tile_pool(name="o_pool", bufs=4) as o_pool,
+        tc.tile_pool(name="quant", bufs=3) as quant,
+        tc.tile_pool(name="work", bufs=3) as work,
+        tc.tile_pool(name="unread", bufs=4) as unread,
+        tc.tile_pool(name="stats", bufs=4) as stats,
+        tc.psum_pool(name="xt_pool", bufs=2) as xt_pool,
+        tc.psum_pool(name="acc_pool", bufs=6) as acc_pool,
+    ):
+        w_scales = consts.tile([P, BANKS * PASSES, D], U8, align_bytes=64)
+        nc.vector.memset(w_scales[:].bitcast(I32), 0)
+        scale_rows = pt_w_scales.bitcast(I32)
+        for b in range(2):
+            for r in range(4):
+                nc.sync.dma_start(
+                    out=w_scales[32 * b + r : P : 64, :, :].bitcast(I32),
+                    in_=scale_rows[:, 4 * b + r : 16 : 8, :].rearrange("g c n -> c g n"),
+                )
+        w_words = consts.tile([P, BANKS * PASSES, 2 * D], U8, align_bytes=64)
+
+        gain = consts.tile([P, BANKS, D], BF16)
+        bias = consts.tile([P, BANKS, D], BF16)
+        nc.scalar.dma_start(
+            out=bias[:].rearrange("p n d -> p (n d)"),
+            in_=pln_b.rearrange("n d -> (n d)").partition_broadcast(P),
+        )
+        nc.scalar.dma_start(
+            out=gain[:].rearrange("p n d -> p (n d)"),
+            in_=pln_g.rearrange("n d -> (n d)").partition_broadcast(P),
+        )
+
+        ident = consts.tile([P, P], F32)
+        make_identity(nc, ident[:])
+        minus_half = consts.tile([P, PAIR], F32)
+        nc.gpsimd.memset(minus_half[:], -0.5)
+
+        x_tiles = {}
+        pw_tiles = {}
+        mx_rows = {}
+
+        def load(c):
+            bank, first = c // CHUNKS_PER_BANK, PAIR * (c % CHUNKS_PER_BANK)
+            x_c = x_pool.tile([P, PAIR, K], BF16)
+            nc.sync.dma_start(out=x_c[:], in_=x_rows[bank, :, first : first + PAIR, :])
+            if first == 0:
+                for g in range(bank * PASSES, (bank + 1) * PASSES):
+                    nc.sync.dma_start(
+                        out=w_words[:, g, :].bitcast(I32), in_=pt_w_words[g].bitcast(I32)
+                    )
+            pw_c = pw_pool.tile([P, PAIR, D], BF16)
+            nc.sync.dma_start(out=pw_c[:], in_=pw_rows[bank, :, first : first + PAIR, :])
+            x_tiles[c] = x_c
+            pw_tiles[c] = pw_c
+
+        def transpose_and_quantise(c):
+            x_c = x_tiles[c]
+            grouped = quant.tile([P, PAIR, K], BF16, align_bytes=64)
+            for j in range(PAIR):
+                x_words = x_c[:, j, :].bitcast(F32)
+                xt = xt_pool.tile([P, PASSES, 2, P], F32)
+                for s in range(PASSES):
+                    for u in range(2):
+                        nc.tensor.transpose(
+                            xt[:, s, u, :],
+                            x_words[:, 2 * P * s + u : 2 * P * (s + 1) : 2],
+                            ident[:],
+                        )
+                nc.scalar.copy(
+                    out=grouped[:, j, :]
+                    .bitcast(F32)
+                    .rearrange("p (s r u) -> p s r u", s=PASSES, u=2),
+                    in_=xt[:].rearrange("p s u r -> p s r u"),
+                )
+            codes = quant.tile([P, PAIR * PASSES * P], U32, align_bytes=64)
+            scales = quant.tile([P, PAIR * PASSES * P], U8, align_bytes=64)
+            nc.vector.quantize_mx(
+                out=codes[:].bitcast(FP8X4),
+                scales=scales[:],
+                in_=grouped[:].rearrange("p j k -> p (j k)"),
+            )
+            mx_rows[c] = (codes, scales)
+
+        def multiply(c, j):
+            bank = c // CHUNKS_PER_BANK
+            codes, scales = mx_rows[c]
+            banks_of_tile = []
+            for h in range(HALVES):
+                acc = acc_pool.tile([P, HALF], F32)
+                for s in range(PASSES):
+                    rows = slice((j * PASSES + s) * P, (j * PASSES + s + 1) * P)
+                    g = bank * PASSES + s
+                    nc.tensor.matmul_mx(
+                        out=acc[:],
+                        lhsT=codes[:, rows].bitcast(FP8X4),
+                        lhsT_scale=scales[:, rows],
+                        rhs=w_words[:, g, 2 * HALF * h : 2 * HALF * (h + 1)].bitcast(FP4X4),
+                        rhs_scale=w_scales[:, g, HALF * h : HALF * (h + 1)],
+                        start=(s == 0),
+                        stop=(s == PASSES - 1),
+                    )
+                banks_of_tile.append(acc)
+            return banks_of_tile
+
+        def sum_over_features(x_psum, func, shift, scale):
+            sums = stats.tile([P, PAIR, HALVES], F32)
+            for j in range(PAIR):
+                for h in range(HALVES):
+                    dropped = unread.tile([P, HALF], BF16)
+                    nc.scalar.activation(
+                        out=dropped[:],
+                        in_=x_psum[j][h][:],
+                        func=func,
+                        bias=0.0 if shift is None else shift[:, j : j + 1],
+                        scale=scale,
+                        accum_out=sums[:, j, h : h + 1],
+                    )
+            return sums
+
+        for c in range(LOADS_AHEAD):
+            load(c)
+        transpose_and_quantise(0)
+
+        for c in range(CHUNKS):
+            bank, first = c // CHUNKS_PER_BANK, PAIR * (c % CHUNKS_PER_BANK)
+            if c + LOADS_AHEAD < CHUNKS:
+                load(c + LOADS_AHEAD)
+            if c + 1 < CHUNKS:
+                transpose_and_quantise(c + 1)
+
+            o_c = o_pool.tile([P, PAIR, D], F32)
+            nc.vector.tensor_tensor(
+                out=o_c[:],
+                in0=pw_tiles[c][:],
+                in1=bias[:, bank, :].unsqueeze(1).to_broadcast([P, PAIR, D]),
+                op=ALU.add,
+            )
+
+            x_psum = [multiply(c, j) for j in range(PAIR)]
+
+            part_negmean = sum_over_features(x_psum, ACT.Copy, None, -1.0 / D)
+            negmean = stats.tile([P, PAIR], F32)
+            nc.gpsimd.tensor_tensor(
+                out=negmean[:], in0=part_negmean[:, :, 0], in1=part_negmean[:, :, 1], op=ALU.add
+            )
+            part_sq = sum_over_features(x_psum, ACT.Square, negmean, 1.0)
+            sq = stats.tile([P, PAIR], F32)
+            nc.gpsimd.tensor_tensor(
+                out=sq[:], in0=part_sq[:, :, 0], in1=part_sq[:, :, 1], op=ALU.add
+            )
+            var_eps = stats.tile([P, PAIR], F32)
+            nc.gpsimd.tensor_scalar(
+                out=var_eps[:], in0=sq[:], scalar1=1.0 / D, scalar2=LN_EPS, op0=ALU.mult, op1=ALU.add
+            )
+            rstd = stats.tile([P, PAIR], F32)
+            nc.gpsimd.tensor_tensor(out=rstd[:], in0=var_eps[:], in1=minus_half[:], op=ALU.pow)
+
+            for j in range(PAIR):
+                centred_gain = work.tile([P, D], F32)
+                for h in range(HALVES):
+                    cols = slice(HALF * h, HALF * (h + 1))
+                    nc.vector.scalar_tensor_tensor(
+                        out=centred_gain[:, cols],
+                        in0=x_psum[j][h][:],
+                        scalar=negmean[:, j : j + 1],
+                        in1=gain[:, bank, cols],
+                        op0=ALU.add,
+                        op1=ALU.mult,
+                    )
+                nc.vector.scalar_tensor_tensor(
+                    out=o_c[:, j, :],
+                    in0=centred_gain[:],
+                    scalar=rstd[:, j : j + 1],
+                    in1=o_c[:, j, :],
+                    op0=ALU.mult,
+                    op1=ALU.add,
+                )
+                nc.sync.dma_start(out=out_rows[bank, :, first + j, :], in_=o_c[:, j, :])

@@ -40,68 +40,92 @@ def tile_moietransformerblock_pb_e_kernel(
     pw_rows = proto_w.rearrange("n (p t) d -> n p t d", t=ROW_TILES)
     out_rows = out.rearrange("n (p t) d -> n p t d", t=ROW_TILES)
 
+    def bank_of(c):
+        return c // CHUNKS_PER_BANK
+
+    def first_tile_of(c):
+        return PAIR * (c % CHUNKS_PER_BANK)
+
+    def exists(c):
+        return 0 <= c < CHUNKS
+
     with (
         tc.tile_pool(name="consts", bufs=1) as consts,
         tc.tile_pool(name="x_pool", bufs=LOADS_AHEAD + 1) as x_pool,
-        tc.tile_pool(name="pw_pool", bufs=LOADS_AHEAD + 1) as pw_pool,
+        tc.tile_pool(name="pw_pool", bufs=LOADS_AHEAD + 3) as pw_pool,
         tc.tile_pool(name="o_pool", bufs=4) as o_pool,
-        tc.tile_pool(name="quant", bufs=3) as quant,
-        tc.tile_pool(name="work", bufs=3) as work,
+        tc.tile_pool(name="quant", bufs=2) as quant,
         tc.tile_pool(name="unread", bufs=4) as unread,
-        tc.tile_pool(name="stats", bufs=4) as stats,
-        tc.psum_pool(name="xt_pool", bufs=2) as xt_pool,
-        tc.psum_pool(name="acc_pool", bufs=6) as acc_pool,
+        tc.tile_pool(name="stats", bufs=3) as stats,
+        tc.psum_pool(name="xt_pool", bufs=PAIR) as xt_pool,
+        tc.psum_pool(name="acc_pool", bufs=PAIR * HALVES) as acc_pool,
+        tc.psum_pool(name="bias_pool", bufs=1) as bias_pool,
+        tc.manual_schedule(),
     ):
+        x_tiles, pw_tiles, xt_tiles, grouped_tiles, mx_rows = {}, {}, {}, {}, {}
+        x_psum, part_negmean, negmean, part_sq, sq, std, o_tiles = {}, {}, {}, {}, {}, {}, {}
+        bias_psum = {}
+
         w_scales = consts.tile([P, BANKS * PASSES, D], U8, align_bytes=64)
         nc.vector.memset(w_scales[:].bitcast(I32), 0)
-        scale_rows = pt_w_scales.bitcast(I32)
-        for b in range(2):
-            for r in range(4):
-                nc.sync.dma_start(
-                    out=w_scales[32 * b + r : P : 64, :, :].bitcast(I32),
-                    in_=scale_rows[:, 4 * b + r : 16 : 8, :].rearrange("g c n -> c g n"),
-                )
         w_words = consts.tile([P, BANKS * PASSES, 2 * D], U8, align_bytes=64)
 
-        gain = consts.tile([P, BANKS, D], BF16)
-        bias = consts.tile([P, BANKS, D], BF16)
+        bias_rows = consts.tile([P, BANKS, D], BF16)
+        nc.vector.memset(bias_rows[:].bitcast(I32), 0)
+        ones = consts.tile([P, P], BF16)
+        nc.vector.memset(ones[:], 1.0)
+        eps = consts.tile([P, 1], F32)
+        nc.vector.memset(eps[:], LN_EPS)
         nc.scalar.dma_start(
-            out=bias[:].rearrange("p n d -> p (n d)"),
-            in_=pln_b.rearrange("n d -> (n d)").partition_broadcast(P),
+            out=bias_rows[0:1, :, :].rearrange("o n d -> o (n d)"),
+            in_=pln_b.rearrange("n d -> (n d)").unsqueeze(0),
         )
+        gain = consts.tile([P, BANKS, D], BF16)
         nc.scalar.dma_start(
             out=gain[:].rearrange("p n d -> p (n d)"),
             in_=pln_g.rearrange("n d -> (n d)").partition_broadcast(P),
         )
+        first_sqrt = consts.tile([P, 1], F32)
+        nc.scalar.activation(out=first_sqrt[:], in_=eps[:], func=ACT.Sqrt)
 
         ident = consts.tile([P, P], F32)
         make_identity(nc, ident[:])
-        minus_half = consts.tile([P, PAIR], F32)
-        nc.gpsimd.memset(minus_half[:], -0.5)
 
-        x_tiles = {}
-        pw_tiles = {}
-        mx_rows = {}
-
-        def load(c):
-            bank, first = c // CHUNKS_PER_BANK, PAIR * (c % CHUNKS_PER_BANK)
+        def load_x(c):
+            if not exists(c):
+                return
+            first = first_tile_of(c)
             x_c = x_pool.tile([P, PAIR, K], BF16)
-            nc.sync.dma_start(out=x_c[:], in_=x_rows[bank, :, first : first + PAIR, :])
+            nc.sync.dma_start(out=x_c[:], in_=x_rows[bank_of(c), :, first : first + PAIR, :])
+            x_tiles[c] = x_c
             if first == 0:
-                for g in range(bank * PASSES, (bank + 1) * PASSES):
+                for g in range(bank_of(c) * PASSES, (bank_of(c) + 1) * PASSES):
                     nc.sync.dma_start(
                         out=w_words[:, g, :].bitcast(I32), in_=pt_w_words[g].bitcast(I32)
                     )
+
+        def load_weight_scales():
+            scale_rows = pt_w_scales.bitcast(I32)
+            for b in range(2):
+                for r in range(4):
+                    nc.sync.dma_start(
+                        out=w_scales[32 * b + r : P : 64, :, :].bitcast(I32),
+                        in_=scale_rows[:, 4 * b + r : 16 : 8, :].rearrange("g c n -> c g n"),
+                    )
+
+        def load_proto_w(c):
+            if not exists(c):
+                return
+            first = first_tile_of(c)
             pw_c = pw_pool.tile([P, PAIR, D], BF16)
-            nc.sync.dma_start(out=pw_c[:], in_=pw_rows[bank, :, first : first + PAIR, :])
-            x_tiles[c] = x_c
+            nc.sync.dma_start(out=pw_c[:], in_=pw_rows[bank_of(c), :, first : first + PAIR, :])
             pw_tiles[c] = pw_c
 
-        def transpose_and_quantise(c):
-            x_c = x_tiles[c]
-            grouped = quant.tile([P, PAIR, K], BF16, align_bytes=64)
+        def transpose(c):
+            if not exists(c):
+                return
             for j in range(PAIR):
-                x_words = x_c[:, j, :].bitcast(F32)
+                x_words = x_tiles[c][:, j, :].bitcast(F32)
                 xt = xt_pool.tile([P, PASSES, 2, P], F32)
                 for s in range(PASSES):
                     for u in range(2):
@@ -110,113 +134,184 @@ def tile_moietransformerblock_pb_e_kernel(
                             x_words[:, 2 * P * s + u : 2 * P * (s + 1) : 2],
                             ident[:],
                         )
+                xt_tiles[c, j] = xt
+
+        def regroup(c):
+            if not exists(c):
+                return
+            grouped = quant.tile([P, PAIR, K], BF16, align_bytes=64)
+            for j in range(PAIR):
                 nc.scalar.copy(
                     out=grouped[:, j, :]
                     .bitcast(F32)
                     .rearrange("p (s r u) -> p s r u", s=PASSES, u=2),
-                    in_=xt[:].rearrange("p s u r -> p s r u"),
+                    in_=xt_tiles[c, j][:].rearrange("p s u r -> p s r u"),
                 )
+            grouped_tiles[c] = grouped
+
+        def quantise(c):
+            if not exists(c):
+                return
             codes = quant.tile([P, PAIR * PASSES * P], U32, align_bytes=64)
             scales = quant.tile([P, PAIR * PASSES * P], U8, align_bytes=64)
             nc.vector.quantize_mx(
                 out=codes[:].bitcast(FP8X4),
                 scales=scales[:],
-                in_=grouped[:].rearrange("p j k -> p (j k)"),
+                in_=grouped_tiles[c][:].rearrange("p j k -> p (j k)"),
             )
             mx_rows[c] = (codes, scales)
 
-        def multiply(c, j):
-            bank = c // CHUNKS_PER_BANK
+        def multiply(c):
+            if not exists(c):
+                return
             codes, scales = mx_rows[c]
-            banks_of_tile = []
-            for h in range(HALVES):
-                acc = acc_pool.tile([P, HALF], F32)
-                for s in range(PASSES):
-                    rows = slice((j * PASSES + s) * P, (j * PASSES + s + 1) * P)
-                    g = bank * PASSES + s
-                    nc.tensor.matmul_mx(
-                        out=acc[:],
-                        lhsT=codes[:, rows].bitcast(FP8X4),
-                        lhsT_scale=scales[:, rows],
-                        rhs=w_words[:, g, 2 * HALF * h : 2 * HALF * (h + 1)].bitcast(FP4X4),
-                        rhs_scale=w_scales[:, g, HALF * h : HALF * (h + 1)],
-                        start=(s == 0),
-                        stop=(s == PASSES - 1),
-                    )
-                banks_of_tile.append(acc)
-            return banks_of_tile
-
-        def sum_over_features(x_psum, func, shift, scale):
-            sums = stats.tile([P, PAIR, HALVES], F32)
             for j in range(PAIR):
                 for h in range(HALVES):
-                    dropped = unread.tile([P, HALF], BF16)
-                    nc.scalar.activation(
-                        out=dropped[:],
-                        in_=x_psum[j][h][:],
-                        func=func,
-                        bias=0.0 if shift is None else shift[:, j : j + 1],
-                        scale=scale,
-                        accum_out=sums[:, j, h : h + 1],
-                    )
-            return sums
+                    acc = acc_pool.tile([P, HALF], F32)
+                    for s in range(PASSES):
+                        rows = slice((j * PASSES + s) * P, (j * PASSES + s + 1) * P)
+                        g = bank_of(c) * PASSES + s
+                        nc.tensor.matmul_mx(
+                            out=acc[:],
+                            lhsT=codes[:, rows].bitcast(FP8X4),
+                            lhsT_scale=scales[:, rows],
+                            rhs=w_words[:, g, 2 * HALF * h : 2 * HALF * (h + 1)].bitcast(FP4X4),
+                            rhs_scale=w_scales[:, g, HALF * h : HALF * (h + 1)],
+                            start=(s == 0),
+                            stop=(s == PASSES - 1),
+                        )
+                    x_psum[c, j, h] = acc
 
-        for c in range(LOADS_AHEAD):
-            load(c)
-        transpose_and_quantise(0)
+        def spread_bias(c):
+            if not exists(c) or first_tile_of(c) != 0:
+                return
+            for h in range(HALVES):
+                spread = bias_pool.tile([P, HALF], F32, name="bias_half%d" % h)
+                nc.tensor.matmul(
+                    out=spread[:],
+                    lhsT=ones[:],
+                    rhs=bias_rows[:, bank_of(c), HALF * h : HALF * (h + 1)],
+                    start=True,
+                    stop=True,
+                )
+                bias_psum[h] = spread
 
-        for c in range(CHUNKS):
-            bank, first = c // CHUNKS_PER_BANK, PAIR * (c % CHUNKS_PER_BANK)
-            if c + LOADS_AHEAD < CHUNKS:
-                load(c + LOADS_AHEAD)
-            if c + 1 < CHUNKS:
-                transpose_and_quantise(c + 1)
+        def sum_over_features(sums, c, j, func, shift, scale):
+            for h in range(HALVES):
+                dropped = unread.tile([P, HALF], BF16)
+                nc.scalar.activation(
+                    out=dropped[:],
+                    in_=x_psum[c, j, h][:],
+                    func=func,
+                    bias=shift,
+                    scale=scale,
+                    accum_out=sums[:, j, h : h + 1],
+                )
 
-            o_c = o_pool.tile([P, PAIR, D], F32)
-            nc.vector.tensor_tensor(
-                out=o_c[:],
-                in0=pw_tiles[c][:],
-                in1=bias[:, bank, :].unsqueeze(1).to_broadcast([P, PAIR, D]),
-                op=ALU.add,
+        def sum_for_mean(c, j):
+            if not exists(c):
+                return
+            if j == 0:
+                part_negmean[c] = stats.tile([P, PAIR, HALVES], F32, name="part_negmean")
+            sum_over_features(part_negmean[c], c, j, ACT.Copy, 0.0, -1.0 / D)
+
+        def join_mean(c):
+            if not exists(c):
+                return
+            negmean[c] = stats.tile([P, PAIR], F32, name="negmean")
+            nc.vector.tensor_reduce(
+                out=negmean[c][:], in_=part_negmean[c][:], axis=mybir.AxisListType.X, op=ALU.add
             )
 
-            x_psum = [multiply(c, j) for j in range(PAIR)]
+        def sum_for_variance(c, j):
+            if not exists(c):
+                return
+            if j == 0:
+                part_sq[c] = stats.tile([P, PAIR, HALVES], F32, name="part_sq")
+            sum_over_features(part_sq[c], c, j, ACT.Square, negmean[c][:, j : j + 1], 1.0)
 
-            part_negmean = sum_over_features(x_psum, ACT.Copy, None, -1.0 / D)
-            negmean = stats.tile([P, PAIR], F32)
-            nc.gpsimd.tensor_tensor(
-                out=negmean[:], in0=part_negmean[:, :, 0], in1=part_negmean[:, :, 1], op=ALU.add
+        def join_variance(c):
+            if not exists(c):
+                return
+            sq[c] = stats.tile([P, PAIR], F32, name="sq")
+            nc.vector.tensor_reduce(
+                out=sq[c][:], in_=part_sq[c][:], axis=mybir.AxisListType.X, op=ALU.add
             )
-            part_sq = sum_over_features(x_psum, ACT.Square, negmean, 1.0)
-            sq = stats.tile([P, PAIR], F32)
-            nc.gpsimd.tensor_tensor(
-                out=sq[:], in0=part_sq[:, :, 0], in1=part_sq[:, :, 1], op=ALU.add
+
+        def root(c):
+            if not exists(c):
+                return
+            std[c] = stats.tile([P, PAIR], F32, name="std")
+            nc.scalar.activation(
+                out=std[c][:], in_=sq[c][:], func=ACT.Sqrt, bias=eps[:, 0:1], scale=1.0 / D
             )
-            var_eps = stats.tile([P, PAIR], F32)
-            nc.gpsimd.tensor_scalar(
-                out=var_eps[:], in0=sq[:], scalar1=1.0 / D, scalar2=LN_EPS, op0=ALU.mult, op1=ALU.add
-            )
+
+        def centre_times_gain(c, j):
+            if not exists(c):
+                return
+            if j == 0:
+                o_tiles[c] = o_pool.tile([P, PAIR, D], F32, name="o_c")
+            for h in range(HALVES):
+                cols = slice(HALF * h, HALF * (h + 1))
+                nc.vector.scalar_tensor_tensor(
+                    out=o_tiles[c][:, j, cols],
+                    in0=x_psum[c, j, h][:],
+                    scalar=negmean[c][:, j : j + 1],
+                    in1=gain[:, bank_of(c), cols],
+                    op0=ALU.add,
+                    op1=ALU.mult,
+                )
+
+        def finish(c):
+            if not exists(c):
+                return
             rstd = stats.tile([P, PAIR], F32)
-            nc.gpsimd.tensor_tensor(out=rstd[:], in0=var_eps[:], in1=minus_half[:], op=ALU.pow)
-
+            nc.vector.reciprocal(out=rstd[:], in_=std[c][:])
+            o_c = o_tiles[c]
             for j in range(PAIR):
-                centred_gain = work.tile([P, D], F32)
                 for h in range(HALVES):
                     cols = slice(HALF * h, HALF * (h + 1))
                     nc.vector.scalar_tensor_tensor(
-                        out=centred_gain[:, cols],
-                        in0=x_psum[j][h][:],
-                        scalar=negmean[:, j : j + 1],
-                        in1=gain[:, bank, cols],
-                        op0=ALU.add,
-                        op1=ALU.mult,
+                        out=o_c[:, j, cols],
+                        in0=o_c[:, j, cols],
+                        scalar=rstd[:, j : j + 1],
+                        in1=bias_psum[h][:],
+                        op0=ALU.mult,
+                        op1=ALU.add,
                     )
-                nc.vector.scalar_tensor_tensor(
-                    out=o_c[:, j, :],
-                    in0=centred_gain[:],
-                    scalar=rstd[:, j : j + 1],
-                    in1=o_c[:, j, :],
-                    op0=ALU.mult,
-                    op1=ALU.add,
+                nc.gpsimd.tensor_tensor(
+                    out=o_c[:, j, :], in0=o_c[:, j, :], in1=pw_tiles[c][:, j, :], op=ALU.add
                 )
-                nc.sync.dma_start(out=out_rows[bank, :, first + j, :], in_=o_c[:, j, :])
+                nc.sync.dma_start(
+                    out=out_rows[bank_of(c), :, first_tile_of(c) + j, :], in_=o_c[:, j, :]
+                )
+
+        load_x(0)
+        load_weight_scales()
+        load_x(1)
+        load_proto_w(0)
+        load_x(2)
+        load_proto_w(1)
+        load_proto_w(2)
+        transpose(0)
+        regroup(0)
+        quantise(0)
+        transpose(1)
+        for c in range(CHUNKS + 1):
+            load_x(c + LOADS_AHEAD)
+            load_proto_w(c + LOADS_AHEAD)
+            join_variance(c - 1)
+            multiply(c)
+            spread_bias(c - 1)
+            sum_for_mean(c, 0)
+            sum_for_mean(c, 1)
+            regroup(c + 1)
+            transpose(c + 2)
+            root(c - 1)
+            join_mean(c)
+            centre_times_gain(c, 0)
+            quantise(c + 1)
+            centre_times_gain(c, 1)
+            sum_for_variance(c, 0)
+            sum_for_variance(c, 1)
+            finish(c - 1)

@@ -26,7 +26,8 @@ ROW_TILES = ROWS // P
 PAIR = 2
 CHUNKS_PER_BANK = ROW_TILES // PAIR
 CHUNKS = BANKS * CHUNKS_PER_BANK
-LOADS_AHEAD = 3
+X_AHEAD = 4
+PW_AHEAD = 2
 
 FLOPS = 2 * BANKS * ROWS * K * D
 
@@ -51,39 +52,41 @@ def tile_moietransformerblock_pb_e_kernel(
 
     with (
         tc.tile_pool(name="consts", bufs=1) as consts,
-        tc.tile_pool(name="x_pool", bufs=LOADS_AHEAD + 1) as x_pool,
-        tc.tile_pool(name="pw_pool", bufs=LOADS_AHEAD + 3) as pw_pool,
+        tc.tile_pool(name="x_pool", bufs=X_AHEAD + 1) as x_pool,
+        tc.tile_pool(name="pw_pool", bufs=PW_AHEAD + 4) as pw_pool,
+        tc.tile_pool(name="quant", bufs=3) as quant,
+        tc.tile_pool(name="y_pool", bufs=3) as y_pool,
         tc.tile_pool(name="o_pool", bufs=4) as o_pool,
-        tc.tile_pool(name="quant", bufs=2) as quant,
-        tc.tile_pool(name="unread", bufs=4) as unread,
+        tc.tile_pool(name="unread", bufs=2) as unread,
         tc.tile_pool(name="stats", bufs=3) as stats,
         tc.psum_pool(name="xt_pool", bufs=PAIR) as xt_pool,
+        tc.psum_pool(name="spread_pool", bufs=1) as spread_pool,
         tc.psum_pool(name="acc_pool", bufs=PAIR * HALVES) as acc_pool,
-        tc.psum_pool(name="bias_pool", bufs=1) as bias_pool,
         tc.manual_schedule(),
     ):
-        x_tiles, pw_tiles, xt_tiles, grouped_tiles, mx_rows = {}, {}, {}, {}, {}
-        x_psum, part_negmean, negmean, part_sq, sq, std, o_tiles = {}, {}, {}, {}, {}, {}, {}
-        bias_psum = {}
+        x_tiles, pw_tiles, xt_tiles, grouped_tiles, mx_rows, x_psum = {}, {}, {}, {}, {}, {}
+        y_tiles, part_sum, negmean, sq, std, o_tiles = {}, {}, {}, {}, {}, {}
+        gain_psum, bias_psum = {}, {}
 
         w_scales = consts.tile([P, BANKS * PASSES, D], U8, align_bytes=64)
         nc.vector.memset(w_scales[:].bitcast(I32), 0)
         w_words = consts.tile([P, BANKS * PASSES, 2 * D], U8, align_bytes=64)
 
-        bias_rows = consts.tile([P, BANKS, D], BF16)
-        nc.vector.memset(bias_rows[:].bitcast(I32), 0)
-        ones = consts.tile([P, P], BF16)
-        nc.vector.memset(ones[:], 1.0)
         eps = consts.tile([P, 1], F32)
         nc.vector.memset(eps[:], LN_EPS)
+        ones = consts.tile([P, P], BF16)
+        nc.vector.memset(ones[:], 1.0)
+        gain_rows = consts.tile([P, BANKS, D], BF16)
+        nc.vector.memset(gain_rows[:].bitcast(I32), 0)
+        bias_rows = consts.tile([P, BANKS, D], BF16)
+        nc.vector.memset(bias_rows[:].bitcast(I32), 0)
+        nc.scalar.dma_start(
+            out=gain_rows[0:1, :, :].rearrange("o n d -> o (n d)"),
+            in_=pln_g.rearrange("n d -> (n d)").unsqueeze(0),
+        )
         nc.scalar.dma_start(
             out=bias_rows[0:1, :, :].rearrange("o n d -> o (n d)"),
             in_=pln_b.rearrange("n d -> (n d)").unsqueeze(0),
-        )
-        gain = consts.tile([P, BANKS, D], BF16)
-        nc.scalar.dma_start(
-            out=gain[:].rearrange("p n d -> p (n d)"),
-            in_=pln_g.rearrange("n d -> (n d)").partition_broadcast(P),
         )
         first_sqrt = consts.tile([P, 1], F32)
         nc.scalar.activation(out=first_sqrt[:], in_=eps[:], func=ACT.Sqrt)
@@ -182,61 +185,67 @@ def tile_moietransformerblock_pb_e_kernel(
                         )
                     x_psum[c, j, h] = acc
 
-        def spread_bias(c):
-            if not exists(c) or first_tile_of(c) != 0:
-                return
+        def spread(c, rows_of_banks, name):
+            wide = spread_pool.tile([P, D], BF16, name=name)
             for h in range(HALVES):
-                spread = bias_pool.tile([P, HALF], F32, name="bias_half%d" % h)
+                cols = slice(HALF * h, HALF * (h + 1))
                 nc.tensor.matmul(
-                    out=spread[:],
+                    out=wide[:, cols],
                     lhsT=ones[:],
-                    rhs=bias_rows[:, bank_of(c), HALF * h : HALF * (h + 1)],
+                    rhs=rows_of_banks[:, bank_of(c), cols],
                     start=True,
                     stop=True,
                 )
-                bias_psum[h] = spread
+            return wide
 
-        def sum_over_features(sums, c, j, func, shift, scale):
-            for h in range(HALVES):
-                dropped = unread.tile([P, HALF], BF16)
-                nc.scalar.activation(
-                    out=dropped[:],
-                    in_=x_psum[c, j, h][:],
-                    func=func,
-                    bias=shift,
-                    scale=scale,
-                    accum_out=sums[:, j, h : h + 1],
-                )
+        def spread_gain(c):
+            if exists(c) and first_tile_of(c) == 0:
+                gain_psum[bank_of(c)] = spread(c, gain_rows, "gain_wide")
 
-        def sum_for_mean(c, j):
+        def spread_bias(c):
+            if exists(c) and first_tile_of(c) == 0:
+                bias_psum[bank_of(c)] = spread(c, bias_rows, "bias_wide")
+
+        def copy_and_sum(c):
             if not exists(c):
                 return
-            if j == 0:
-                part_negmean[c] = stats.tile([P, PAIR, HALVES], F32, name="part_negmean")
-            sum_over_features(part_negmean[c], c, j, ACT.Copy, 0.0, -1.0 / D)
+            y_c = y_pool.tile([P, PAIR, D], F32)
+            sums = stats.tile([P, PAIR, HALVES], F32)
+            for j in range(PAIR):
+                for h in range(HALVES):
+                    nc.scalar.activation(
+                        out=y_c[:, j, HALF * h : HALF * (h + 1)],
+                        in_=x_psum[c, j, h][:],
+                        func=ACT.Copy,
+                        accum_out=sums[:, j, h : h + 1],
+                    )
+            y_tiles[c] = y_c
+            part_sum[c] = sums
 
         def join_mean(c):
             if not exists(c):
                 return
-            negmean[c] = stats.tile([P, PAIR], F32, name="negmean")
+            total = stats.tile([P, PAIR], F32)
             nc.vector.tensor_reduce(
-                out=negmean[c][:], in_=part_negmean[c][:], axis=mybir.AxisListType.X, op=ALU.add
+                out=total[:], in_=part_sum[c][:], axis=mybir.AxisListType.X, op=ALU.add
             )
+            negmean[c] = stats.tile([P, PAIR], F32, name="negmean")
+            nc.vector.tensor_scalar_mul(out=negmean[c][:], in0=total[:], scalar1=-1.0 / D)
 
-        def sum_for_variance(c, j):
-            if not exists(c):
-                return
-            if j == 0:
-                part_sq[c] = stats.tile([P, PAIR, HALVES], F32, name="part_sq")
-            sum_over_features(part_sq[c], c, j, ACT.Square, negmean[c][:, j : j + 1], 1.0)
-
-        def join_variance(c):
+        def sum_squares(c):
             if not exists(c):
                 return
             sq[c] = stats.tile([P, PAIR], F32, name="sq")
-            nc.vector.tensor_reduce(
-                out=sq[c][:], in_=part_sq[c][:], axis=mybir.AxisListType.X, op=ALU.add
-            )
+            for j in range(PAIR):
+                dropped = unread.tile([P, D], BF16)
+                nc.scalar.activation(
+                    out=dropped[:],
+                    in_=y_tiles[c][:, j, :],
+                    func=ACT.Square,
+                    bias=negmean[c][:, j : j + 1],
+                    scale=1.0,
+                    accum_out=sq[c][:, j : j + 1],
+                )
 
         def root(c):
             if not exists(c):
@@ -246,21 +255,20 @@ def tile_moietransformerblock_pb_e_kernel(
                 out=std[c][:], in_=sq[c][:], func=ACT.Sqrt, bias=eps[:, 0:1], scale=1.0 / D
             )
 
-        def centre_times_gain(c, j):
+        def centre_times_gain(c):
             if not exists(c):
                 return
-            if j == 0:
-                o_tiles[c] = o_pool.tile([P, PAIR, D], F32, name="o_c")
-            for h in range(HALVES):
-                cols = slice(HALF * h, HALF * (h + 1))
+            o_c = o_pool.tile([P, PAIR, D], F32)
+            for j in range(PAIR):
                 nc.vector.scalar_tensor_tensor(
-                    out=o_tiles[c][:, j, cols],
-                    in0=x_psum[c, j, h][:],
+                    out=o_c[:, j, :],
+                    in0=y_tiles[c][:, j, :],
                     scalar=negmean[c][:, j : j + 1],
-                    in1=gain[:, bank_of(c), cols],
+                    in1=gain_psum[bank_of(c)][:],
                     op0=ALU.add,
                     op1=ALU.mult,
                 )
+            o_tiles[c] = o_c
 
         def finish(c):
             if not exists(c):
@@ -269,16 +277,14 @@ def tile_moietransformerblock_pb_e_kernel(
             nc.vector.reciprocal(out=rstd[:], in_=std[c][:])
             o_c = o_tiles[c]
             for j in range(PAIR):
-                for h in range(HALVES):
-                    cols = slice(HALF * h, HALF * (h + 1))
-                    nc.vector.scalar_tensor_tensor(
-                        out=o_c[:, j, cols],
-                        in0=o_c[:, j, cols],
-                        scalar=rstd[:, j : j + 1],
-                        in1=bias_psum[h][:],
-                        op0=ALU.mult,
-                        op1=ALU.add,
-                    )
+                nc.vector.scalar_tensor_tensor(
+                    out=o_c[:, j, :],
+                    in0=o_c[:, j, :],
+                    scalar=rstd[:, j : j + 1],
+                    in1=bias_psum[bank_of(c)][:],
+                    op0=ALU.mult,
+                    op1=ALU.add,
+                )
                 nc.gpsimd.tensor_tensor(
                     out=o_c[:, j, :], in0=o_c[:, j, :], in1=pw_tiles[c][:, j, :], op=ALU.add
                 )
@@ -289,29 +295,30 @@ def tile_moietransformerblock_pb_e_kernel(
         load_x(0)
         load_weight_scales()
         load_x(1)
-        load_proto_w(0)
         load_x(2)
+        load_proto_w(0)
+        load_x(3)
         load_proto_w(1)
-        load_proto_w(2)
         transpose(0)
         regroup(0)
         quantise(0)
         transpose(1)
+        multiply(0)
+        regroup(1)
+        quantise(1)
+        transpose(2)
         for c in range(CHUNKS + 1):
-            load_x(c + LOADS_AHEAD)
-            load_proto_w(c + LOADS_AHEAD)
-            join_variance(c - 1)
-            multiply(c)
-            spread_bias(c - 1)
-            sum_for_mean(c, 0)
-            sum_for_mean(c, 1)
-            regroup(c + 1)
-            transpose(c + 2)
+            load_x(c + X_AHEAD)
+            load_proto_w(c + PW_AHEAD)
             root(c - 1)
-            join_mean(c)
-            centre_times_gain(c, 0)
-            quantise(c + 1)
-            centre_times_gain(c, 1)
-            sum_for_variance(c, 0)
-            sum_for_variance(c, 1)
+            spread_bias(c - 1)
             finish(c - 1)
+            spread_gain(c)
+            copy_and_sum(c)
+            multiply(c + 1)
+            regroup(c + 2)
+            transpose(c + 3)
+            join_mean(c)
+            centre_times_gain(c)
+            quantise(c + 2)
+            sum_squares(c)

@@ -139,18 +139,17 @@ def tile_moietransformerblock_pb_e_kernel(
                         )
                 xt_tiles[c, j] = xt
 
-        def regroup(c):
+        def regroup(c, j, copy):
             if not exists(c):
                 return
-            grouped = quant.tile([P, PAIR, K], BF16, align_bytes=64)
-            for j in range(PAIR):
-                nc.scalar.copy(
-                    out=grouped[:, j, :]
-                    .bitcast(F32)
-                    .rearrange("p (s r u) -> p s r u", s=PASSES, u=2),
-                    in_=xt_tiles[c, j][:].rearrange("p s u r -> p s r u"),
-                )
-            grouped_tiles[c] = grouped
+            if c not in grouped_tiles:
+                grouped_tiles[c] = quant.tile([P, PAIR, K], BF16, align_bytes=64, name="grouped")
+            copy(
+                out=grouped_tiles[c][:, j, :]
+                .bitcast(F32)
+                .rearrange("p (s r u) -> p s r u", s=PASSES, u=2),
+                in_=xt_tiles[c, j][:].rearrange("p s u r -> p s r u"),
+            )
 
         def quantise(c):
             if not exists(c):
@@ -300,23 +299,26 @@ def tile_moietransformerblock_pb_e_kernel(
         load_x(3)
         load_proto_w(1)
         transpose(0)
-        regroup(0)
+        regroup(0, 0, nc.scalar.copy)
+        regroup(0, 1, nc.vector.tensor_copy)
         quantise(0)
         transpose(1)
         multiply(0)
-        regroup(1)
+        regroup(1, 0, nc.scalar.copy)
+        regroup(1, 1, nc.vector.tensor_copy)
         quantise(1)
         transpose(2)
         for c in range(CHUNKS + 1):
             load_x(c + X_AHEAD)
             load_proto_w(c + PW_AHEAD)
+            regroup(c + 2, 1, nc.vector.tensor_copy)
             root(c - 1)
             spread_bias(c - 1)
             finish(c - 1)
             spread_gain(c)
             copy_and_sum(c)
             multiply(c + 1)
-            regroup(c + 2)
+            regroup(c + 2, 0, nc.scalar.copy)
             transpose(c + 3)
             join_mean(c)
             centre_times_gain(c)

@@ -68,38 +68,40 @@ def tile_moietransformerblock_pb_e_kernel(
         y_tiles, part_sum, negmean, sq, std, o_tiles = {}, {}, {}, {}, {}, {}
         gain_psum, bias_psum = {}, {}
 
+        eps = consts.tile([P, 1], F32)
+        nc.vector.memset(eps[:], LN_EPS)
         w_scales = consts.tile([P, BANKS * PASSES, D], U8, align_bytes=64)
         nc.vector.memset(w_scales[:].bitcast(I32), 0)
         w_words = consts.tile([P, BANKS * PASSES, 2 * D], U8, align_bytes=64)
 
-        eps = consts.tile([P, 1], F32)
-        nc.vector.memset(eps[:], LN_EPS)
-        ones = consts.tile([P, P], BF16)
-        nc.vector.memset(ones[:], 1.0)
-        gain_rows = consts.tile([P, BANKS, D], BF16)
-        nc.vector.memset(gain_rows[:].bitcast(I32), 0)
-        bias_rows = consts.tile([P, BANKS, D], BF16)
-        nc.vector.memset(bias_rows[:].bitcast(I32), 0)
-        nc.scalar.dma_start(
-            out=gain_rows[0:1, :, :].rearrange("o n d -> o (n d)"),
-            in_=pln_g.rearrange("n d -> (n d)").unsqueeze(0),
-        )
-        nc.scalar.dma_start(
-            out=bias_rows[0:1, :, :].rearrange("o n d -> o (n d)"),
-            in_=pln_b.rearrange("n d -> (n d)").unsqueeze(0),
-        )
         first_sqrt = consts.tile([P, 1], F32)
         nc.scalar.activation(out=first_sqrt[:], in_=eps[:], func=ACT.Sqrt)
 
         ident = consts.tile([P, P], F32)
         make_identity(nc, ident[:])
 
+        ones = consts.tile([P, P], BF16)
+        nc.vector.memset(ones[:], 1.0)
+        gain_rows = consts.tile([P, BANKS, D], BF16)
+        nc.vector.memset(gain_rows[:].bitcast(I32), 0)
+        bias_rows = consts.tile([P, BANKS, D], BF16)
+        nc.vector.memset(bias_rows[:].bitcast(I32), 0)
+        nc.gpsimd.dma_start(
+            out=gain_rows[0:1, :, :].rearrange("o n d -> o (n d)"),
+            in_=pln_g.rearrange("n d -> (n d)").unsqueeze(0),
+        )
+        nc.gpsimd.dma_start(
+            out=bias_rows[0:1, :, :].rearrange("o n d -> o (n d)"),
+            in_=pln_b.rearrange("n d -> (n d)").unsqueeze(0),
+        )
+
         def load_x(c):
             if not exists(c):
                 return
             first = first_tile_of(c)
             x_c = x_pool.tile([P, PAIR, K], BF16)
-            nc.sync.dma_start(out=x_c[:], in_=x_rows[bank_of(c), :, first : first + PAIR, :])
+            for j in range(PAIR):
+                nc.sync.dma_start(out=x_c[:, j, :], in_=x_rows[bank_of(c), :, first + j, :])
             x_tiles[c] = x_c
             if first == 0:
                 for g in range(bank_of(c) * PASSES, (bank_of(c) + 1) * PASSES):
@@ -139,17 +141,18 @@ def tile_moietransformerblock_pb_e_kernel(
                         )
                 xt_tiles[c, j] = xt
 
-        def regroup(c, j, copy):
+        def regroup(c):
             if not exists(c):
                 return
-            if c not in grouped_tiles:
-                grouped_tiles[c] = quant.tile([P, PAIR, K], BF16, align_bytes=64, name="grouped")
-            copy(
-                out=grouped_tiles[c][:, j, :]
-                .bitcast(F32)
-                .rearrange("p (s r u) -> p s r u", s=PASSES, u=2),
-                in_=xt_tiles[c, j][:].rearrange("p s u r -> p s r u"),
-            )
+            grouped = quant.tile([P, PAIR, K], BF16, align_bytes=64)
+            for j in range(PAIR):
+                nc.scalar.copy(
+                    out=grouped[:, j, :]
+                    .bitcast(F32)
+                    .rearrange("p (s r u) -> p s r u", s=PASSES, u=2),
+                    in_=xt_tiles[c, j][:].rearrange("p s u r -> p s r u"),
+                )
+            grouped_tiles[c] = grouped
 
         def quantise(c):
             if not exists(c):
@@ -272,6 +275,7 @@ def tile_moietransformerblock_pb_e_kernel(
         def finish(c):
             if not exists(c):
                 return
+            last_adder = nc.vector if c == CHUNKS - 1 else nc.gpsimd
             rstd = stats.tile([P, PAIR], F32)
             nc.vector.reciprocal(out=rstd[:], in_=std[c][:])
             o_c = o_tiles[c]
@@ -284,7 +288,8 @@ def tile_moietransformerblock_pb_e_kernel(
                     op0=ALU.mult,
                     op1=ALU.add,
                 )
-                nc.gpsimd.tensor_tensor(
+                adder = last_adder if j == PAIR - 1 else nc.gpsimd
+                adder.tensor_tensor(
                     out=o_c[:, j, :], in0=o_c[:, j, :], in1=pw_tiles[c][:, j, :], op=ALU.add
                 )
                 nc.sync.dma_start(
@@ -299,26 +304,23 @@ def tile_moietransformerblock_pb_e_kernel(
         load_x(3)
         load_proto_w(1)
         transpose(0)
-        regroup(0, 0, nc.scalar.copy)
-        regroup(0, 1, nc.vector.tensor_copy)
+        regroup(0)
         quantise(0)
         transpose(1)
         multiply(0)
-        regroup(1, 0, nc.scalar.copy)
-        regroup(1, 1, nc.vector.tensor_copy)
+        regroup(1)
         quantise(1)
         transpose(2)
         for c in range(CHUNKS + 1):
             load_x(c + X_AHEAD)
             load_proto_w(c + PW_AHEAD)
-            regroup(c + 2, 1, nc.vector.tensor_copy)
             root(c - 1)
             spread_bias(c - 1)
             finish(c - 1)
             spread_gain(c)
             copy_and_sum(c)
             multiply(c + 1)
-            regroup(c + 2, 0, nc.scalar.copy)
+            regroup(c + 2)
             transpose(c + 3)
             join_mean(c)
             centre_times_gain(c)

@@ -75,7 +75,7 @@ def tile_moietransformerblock_pb_e_kernel(
         w_words = consts.tile([P, BANKS * PASSES, 2 * D], U8, align_bytes=64)
 
         first_sqrt = consts.tile([P, 1], F32)
-        nc.scalar.activation(out=first_sqrt[:], in_=eps[:], func=ACT.Sqrt)
+        nc.scalar.activation(out=first_sqrt[:], in_=eps[:], func=ACT.Abs_reciprocal_sqrt)
 
         ident = consts.tile([P, P], F32)
         make_identity(nc, ident[:])
@@ -227,12 +227,18 @@ def tile_moietransformerblock_pb_e_kernel(
         def join_mean(c):
             if not exists(c):
                 return
-            total = stats.tile([P, PAIR], F32)
-            nc.vector.tensor_reduce(
-                out=total[:], in_=part_sum[c][:], axis=mybir.AxisListType.X, op=ALU.add
-            )
+            scaled = stats.tile([P, PAIR, HALVES], F32)
             negmean[c] = stats.tile([P, PAIR], F32, name="negmean")
-            nc.vector.tensor_scalar_mul(out=negmean[c][:], in0=total[:], scalar1=-1.0 / D)
+            for j in range(PAIR):
+                nc.vector.tensor_scalar(
+                    out=scaled[:, j, :],
+                    in0=part_sum[c][:, j, :],
+                    scalar1=-1.0 / D,
+                    scalar2=None,
+                    op0=ALU.mult,
+                    op1=ALU.add,
+                    accum_out=negmean[c][:, j : j + 1],
+                )
 
         def sum_squares(c):
             if not exists(c):
@@ -254,7 +260,11 @@ def tile_moietransformerblock_pb_e_kernel(
                 return
             std[c] = stats.tile([P, PAIR], F32, name="std")
             nc.scalar.activation(
-                out=std[c][:], in_=sq[c][:], func=ACT.Sqrt, bias=eps[:, 0:1], scale=1.0 / D
+                out=std[c][:],
+                in_=sq[c][:],
+                func=ACT.Abs_reciprocal_sqrt,
+                bias=eps[:, 0:1],
+                scale=1.0 / D,
             )
 
         def centre_times_gain(c):
@@ -276,8 +286,7 @@ def tile_moietransformerblock_pb_e_kernel(
             if not exists(c):
                 return
             last_adder = nc.vector if c == CHUNKS - 1 else nc.gpsimd
-            rstd = stats.tile([P, PAIR], F32)
-            nc.vector.reciprocal(out=rstd[:], in_=std[c][:])
+            rstd = std[c]
             o_c = o_tiles[c]
             for j in range(PAIR):
                 nc.vector.scalar_tensor_tensor(

@@ -26,7 +26,7 @@ ROW_TILES = ROWS // P
 PAIR = 2
 CHUNKS_PER_BANK = ROW_TILES // PAIR
 CHUNKS = BANKS * CHUNKS_PER_BANK
-X_AHEAD = 4
+X_AHEAD = 5
 PW_AHEAD = 2
 
 FLOPS = 2 * BANKS * ROWS * K * D
@@ -66,7 +66,7 @@ def tile_moietransformerblock_pb_e_kernel(
     ):
         x_tiles, pw_tiles, xt_tiles, grouped_tiles, mx_rows, x_psum = {}, {}, {}, {}, {}, {}
         y_tiles, part_sum, negmean, sq, std, o_tiles = {}, {}, {}, {}, {}, {}
-        gain_psum, bias_psum = {}, {}
+        gain_psum, bias_psum, scaled = {}, {}, {}
 
         eps = consts.tile([P, 1], F32)
         nc.vector.memset(eps[:], LN_EPS)
@@ -224,21 +224,21 @@ def tile_moietransformerblock_pb_e_kernel(
             y_tiles[c] = y_c
             part_sum[c] = sums
 
-        def join_mean(c):
+        def join_mean(c, j):
             if not exists(c):
                 return
-            scaled = stats.tile([P, PAIR, HALVES], F32)
-            negmean[c] = stats.tile([P, PAIR], F32, name="negmean")
-            for j in range(PAIR):
-                nc.vector.tensor_scalar(
-                    out=scaled[:, j, :],
-                    in0=part_sum[c][:, j, :],
-                    scalar1=-1.0 / D,
-                    scalar2=None,
-                    op0=ALU.mult,
-                    op1=ALU.add,
-                    accum_out=negmean[c][:, j : j + 1],
-                )
+            if j == 0:
+                scaled[c] = stats.tile([P, PAIR, HALVES], F32, name="scaled")
+                negmean[c] = stats.tile([P, PAIR], F32, name="negmean")
+            nc.vector.tensor_scalar(
+                out=scaled[c][:, j, :],
+                in0=part_sum[c][:, j, :],
+                scalar1=-1.0 / D,
+                scalar2=None,
+                op0=ALU.mult,
+                op1=ALU.add,
+                accum_out=negmean[c][:, j : j + 1],
+            )
 
         def sum_squares(c):
             if not exists(c):
@@ -282,28 +282,27 @@ def tile_moietransformerblock_pb_e_kernel(
                 )
             o_tiles[c] = o_c
 
-        def finish(c):
+        def finish(c, j):
             if not exists(c):
                 return
             last_adder = nc.vector if c == CHUNKS - 1 else nc.gpsimd
             rstd = std[c]
             o_c = o_tiles[c]
-            for j in range(PAIR):
-                nc.vector.scalar_tensor_tensor(
-                    out=o_c[:, j, :],
-                    in0=o_c[:, j, :],
-                    scalar=rstd[:, j : j + 1],
-                    in1=bias_psum[bank_of(c)][:],
-                    op0=ALU.mult,
-                    op1=ALU.add,
-                )
-                adder = last_adder if j == PAIR - 1 else nc.gpsimd
-                adder.tensor_tensor(
-                    out=o_c[:, j, :], in0=o_c[:, j, :], in1=pw_tiles[c][:, j, :], op=ALU.add
-                )
-                nc.sync.dma_start(
-                    out=out_rows[bank_of(c), :, first_tile_of(c) + j, :], in_=o_c[:, j, :]
-                )
+            nc.vector.scalar_tensor_tensor(
+                out=o_c[:, j, :],
+                in0=o_c[:, j, :],
+                scalar=rstd[:, j : j + 1],
+                in1=bias_psum[bank_of(c)][:],
+                op0=ALU.mult,
+                op1=ALU.add,
+            )
+            adder = last_adder if j == PAIR - 1 else nc.gpsimd
+            adder.tensor_tensor(
+                out=o_c[:, j, :], in0=o_c[:, j, :], in1=pw_tiles[c][:, j, :], op=ALU.add
+            )
+            nc.sync.dma_start(
+                out=out_rows[bank_of(c), :, first_tile_of(c) + j, :], in_=o_c[:, j, :]
+            )
 
         load_x(0)
         load_weight_scales()
@@ -312,6 +311,7 @@ def tile_moietransformerblock_pb_e_kernel(
         load_proto_w(0)
         load_x(3)
         load_proto_w(1)
+        load_x(4)
         transpose(0)
         regroup(0)
         quantise(0)
@@ -325,13 +325,20 @@ def tile_moietransformerblock_pb_e_kernel(
             load_proto_w(c + PW_AHEAD)
             root(c - 1)
             spread_bias(c - 1)
-            finish(c - 1)
+            finish(c - 1, 0)
+            if c > 0:
+                quantise(c + 2)
             spread_gain(c)
             copy_and_sum(c)
             multiply(c + 1)
-            regroup(c + 2)
-            transpose(c + 3)
-            join_mean(c)
+            if c == 0:
+                regroup(2)
+                transpose(3)
+                quantise(2)
+            join_mean(c, 0)
+            finish(c - 1, 1)
+            join_mean(c, 1)
+            regroup(c + 3)
+            transpose(c + 4)
             centre_times_gain(c)
-            quantise(c + 2)
             sum_squares(c)

@@ -26,7 +26,7 @@ ROW_TILES = ROWS // P
 PAIR = 2
 CHUNKS_PER_BANK = ROW_TILES // PAIR
 CHUNKS = BANKS * CHUNKS_PER_BANK
-X_AHEAD = 5
+X_AHEAD = 4
 PW_AHEAD = 2
 
 FLOPS = 2 * BANKS * ROWS * K * D
@@ -65,13 +65,13 @@ def tile_moietransformerblock_pb_e_kernel(
         tc.manual_schedule(),
     ):
         x_tiles, pw_tiles, xt_tiles, grouped_tiles, mx_rows, x_psum = {}, {}, {}, {}, {}, {}
-        y_tiles, part_sum, negmean, sq, std, o_tiles = {}, {}, {}, {}, {}, {}
+        y_tiles, part_sum, negmean, sq, rstd, o_tiles = {}, {}, {}, {}, {}, {}
         gain_psum, bias_psum, scaled = {}, {}, {}
 
         eps = consts.tile([P, 1], F32)
         nc.vector.memset(eps[:], LN_EPS)
         w_scales = consts.tile([P, BANKS * PASSES, D], U8, align_bytes=64)
-        nc.vector.memset(w_scales[:].bitcast(I32), 0)
+        nc.vector.memset(w_scales[:, 0:PASSES, :].bitcast(I32), 0)
         w_words = consts.tile([P, BANKS * PASSES, 2 * D], U8, align_bytes=64)
 
         first_sqrt = consts.tile([P, 1], F32)
@@ -86,37 +86,43 @@ def tile_moietransformerblock_pb_e_kernel(
         nc.vector.memset(gain_rows[:].bitcast(I32), 0)
         bias_rows = consts.tile([P, BANKS, D], BF16)
         nc.vector.memset(bias_rows[:].bitcast(I32), 0)
-        nc.gpsimd.dma_start(
-            out=gain_rows[0:1, :, :].rearrange("o n d -> o (n d)"),
-            in_=pln_g.rearrange("n d -> (n d)").unsqueeze(0),
-        )
-        nc.gpsimd.dma_start(
-            out=bias_rows[0:1, :, :].rearrange("o n d -> o (n d)"),
-            in_=pln_b.rearrange("n d -> (n d)").unsqueeze(0),
-        )
+        nc.vector.memset(w_scales[:, PASSES:, :].bitcast(I32), 0)
 
-        def load_x(c):
+        def load_x(c, j):
             if not exists(c):
                 return
-            first = first_tile_of(c)
-            x_c = x_pool.tile([P, PAIR, K], BF16)
-            for j in range(PAIR):
-                nc.sync.dma_start(out=x_c[:, j, :], in_=x_rows[bank_of(c), :, first + j, :])
-            x_tiles[c] = x_c
-            if first == 0:
-                for g in range(bank_of(c) * PASSES, (bank_of(c) + 1) * PASSES):
-                    nc.sync.dma_start(
-                        out=w_words[:, g, :].bitcast(I32), in_=pt_w_words[g].bitcast(I32)
-                    )
+            if j == 0:
+                x_tiles[c] = x_pool.tile([P, PAIR, K], BF16, name="x_c")
+            nc.sync.dma_start(
+                out=x_tiles[c][:, j, :], in_=x_rows[bank_of(c), :, first_tile_of(c) + j, :]
+            )
 
-        def load_weight_scales():
+        def load_weight_words(n, h):
+            passes = slice(PASSES * n, PASSES * (n + 1))
+            cols = slice(2 * HALF * h, 2 * HALF * (h + 1))
+            nc.sync.dma_start(
+                out=w_words[:, passes, cols].bitcast(I32),
+                in_=pt_w_words[passes, :, cols].bitcast(I32).rearrange("g p n -> p g n"),
+            )
+
+        def load_weight_scales(n):
+            passes = slice(PASSES * n, PASSES * (n + 1))
             scale_rows = pt_w_scales.bitcast(I32)
-            for b in range(2):
-                for r in range(4):
-                    nc.sync.dma_start(
-                        out=w_scales[32 * b + r : P : 64, :, :].bitcast(I32),
-                        in_=scale_rows[:, 4 * b + r : 16 : 8, :].rearrange("g c n -> c g n"),
-                    )
+            for r in range(4):
+                nc.sync.dma_start(
+                    out=w_scales[r:P:32, passes, :].bitcast(I32),
+                    in_=scale_rows[passes, r:16:4, :].rearrange("g c n -> c g n"),
+                )
+
+        def load_gain_and_bias():
+            nc.sync.dma_start(
+                out=gain_rows[0:1, :, :].rearrange("o n d -> o (n d)"),
+                in_=pln_g.rearrange("n d -> (n d)").unsqueeze(0),
+            )
+            nc.sync.dma_start(
+                out=bias_rows[0:1, :, :].rearrange("o n d -> o (n d)"),
+                in_=pln_b.rearrange("n d -> (n d)").unsqueeze(0),
+            )
 
         def load_proto_w(c):
             if not exists(c):
@@ -126,66 +132,70 @@ def tile_moietransformerblock_pb_e_kernel(
             nc.sync.dma_start(out=pw_c[:], in_=pw_rows[bank_of(c), :, first : first + PAIR, :])
             pw_tiles[c] = pw_c
 
-        def transpose(c):
+        def transpose(c, j):
             if not exists(c):
                 return
-            for j in range(PAIR):
-                x_words = x_tiles[c][:, j, :].bitcast(F32)
-                xt = xt_pool.tile([P, PASSES, 2, P], F32)
-                for s in range(PASSES):
-                    for u in range(2):
-                        nc.tensor.transpose(
-                            xt[:, s, u, :],
-                            x_words[:, 2 * P * s + u : 2 * P * (s + 1) : 2],
-                            ident[:],
-                        )
-                xt_tiles[c, j] = xt
+            x_words = x_tiles[c][:, j, :].bitcast(F32)
+            xt = xt_pool.tile([P, PASSES, 2, P], F32)
+            for s in range(PASSES):
+                for u in range(2):
+                    nc.tensor.transpose(
+                        xt[:, s, u, :],
+                        x_words[:, 2 * P * s + u : 2 * P * (s + 1) : 2],
+                        ident[:],
+                    )
+            xt_tiles[c, j] = xt
 
-        def regroup(c):
+        def regroup(c, j, engine):
             if not exists(c):
                 return
-            grouped = quant.tile([P, PAIR, K], BF16, align_bytes=64)
-            for j in range(PAIR):
-                nc.scalar.copy(
-                    out=grouped[:, j, :]
-                    .bitcast(F32)
-                    .rearrange("p (s r u) -> p s r u", s=PASSES, u=2),
-                    in_=xt_tiles[c, j][:].rearrange("p s u r -> p s r u"),
-                )
-            grouped_tiles[c] = grouped
-
-        def quantise(c):
-            if not exists(c):
-                return
-            codes = quant.tile([P, PAIR * PASSES * P], U32, align_bytes=64)
-            scales = quant.tile([P, PAIR * PASSES * P], U8, align_bytes=64)
-            nc.vector.quantize_mx(
-                out=codes[:].bitcast(FP8X4),
-                scales=scales[:],
-                in_=grouped_tiles[c][:].rearrange("p j k -> p (j k)"),
+            if j == 0:
+                grouped_tiles[c] = quant.tile([P, PAIR, K], BF16, align_bytes=64, name="grouped")
+            side_by_side = (
+                grouped_tiles[c][:, j, :]
+                .bitcast(F32)
+                .rearrange("p (s r u) -> p s r u", s=PASSES, u=2)
             )
-            mx_rows[c] = (codes, scales)
+            transposed = xt_tiles[c, j][:].rearrange("p s u r -> p s r u")
+            if engine == "scalar":
+                nc.scalar.copy(out=side_by_side, in_=transposed)
+            else:
+                nc.vector.tensor_copy(out=side_by_side, in_=transposed)
 
-        def multiply(c):
+        def quantise(c, tiles):
+            if not exists(c):
+                return
+            if tiles.start == 0:
+                codes = quant.tile([P, PAIR * PASSES * P], U32, align_bytes=64)
+                scales = quant.tile([P, PAIR * PASSES * P], U8, align_bytes=64)
+                mx_rows[c] = (codes, scales)
+            codes, scales = mx_rows[c]
+            cols = slice(tiles.start * PASSES * P, tiles.stop * PASSES * P)
+            nc.vector.quantize_mx(
+                out=codes[:, cols].bitcast(FP8X4),
+                scales=scales[:, cols],
+                in_=grouped_tiles[c][:, tiles.start : tiles.stop, :].rearrange("p j k -> p (j k)"),
+            )
+
+        def multiply(c, j):
             if not exists(c):
                 return
             codes, scales = mx_rows[c]
-            for j in range(PAIR):
-                for h in range(HALVES):
-                    acc = acc_pool.tile([P, HALF], F32)
-                    for s in range(PASSES):
-                        rows = slice((j * PASSES + s) * P, (j * PASSES + s + 1) * P)
-                        g = bank_of(c) * PASSES + s
-                        nc.tensor.matmul_mx(
-                            out=acc[:],
-                            lhsT=codes[:, rows].bitcast(FP8X4),
-                            lhsT_scale=scales[:, rows],
-                            rhs=w_words[:, g, 2 * HALF * h : 2 * HALF * (h + 1)].bitcast(FP4X4),
-                            rhs_scale=w_scales[:, g, HALF * h : HALF * (h + 1)],
-                            start=(s == 0),
-                            stop=(s == PASSES - 1),
-                        )
-                    x_psum[c, j, h] = acc
+            for h in range(HALVES):
+                acc = acc_pool.tile([P, HALF], F32)
+                for s in range(PASSES):
+                    rows = slice((j * PASSES + s) * P, (j * PASSES + s + 1) * P)
+                    g = bank_of(c) * PASSES + s
+                    nc.tensor.matmul_mx(
+                        out=acc[:],
+                        lhsT=codes[:, rows].bitcast(FP8X4),
+                        lhsT_scale=scales[:, rows],
+                        rhs=w_words[:, g, 2 * HALF * h : 2 * HALF * (h + 1)].bitcast(FP4X4),
+                        rhs_scale=w_scales[:, g, HALF * h : HALF * (h + 1)],
+                        start=(s == 0),
+                        stop=(s == PASSES - 1),
+                    )
+                x_psum[c, j, h] = acc
 
         def spread(c, rows_of_banks, name):
             wide = spread_pool.tile([P, D], BF16, name=name)
@@ -208,21 +218,19 @@ def tile_moietransformerblock_pb_e_kernel(
             if exists(c) and first_tile_of(c) == 0:
                 bias_psum[bank_of(c)] = spread(c, bias_rows, "bias_wide")
 
-        def copy_and_sum(c):
+        def copy_and_sum(c, j):
             if not exists(c):
                 return
-            y_c = y_pool.tile([P, PAIR, D], F32)
-            sums = stats.tile([P, PAIR, HALVES], F32)
-            for j in range(PAIR):
-                for h in range(HALVES):
-                    nc.scalar.activation(
-                        out=y_c[:, j, HALF * h : HALF * (h + 1)],
-                        in_=x_psum[c, j, h][:],
-                        func=ACT.Copy,
-                        accum_out=sums[:, j, h : h + 1],
-                    )
-            y_tiles[c] = y_c
-            part_sum[c] = sums
+            if j == 0:
+                y_tiles[c] = y_pool.tile([P, PAIR, D], F32, name="y_c")
+                part_sum[c] = stats.tile([P, PAIR, HALVES], F32, name="sums")
+            for h in range(HALVES):
+                nc.scalar.activation(
+                    out=y_tiles[c][:, j, HALF * h : HALF * (h + 1)],
+                    in_=x_psum[c, j, h][:],
+                    func=ACT.Copy,
+                    accum_out=part_sum[c][:, j, h : h + 1],
+                )
 
         def join_mean(c, j):
             if not exists(c):
@@ -240,58 +248,56 @@ def tile_moietransformerblock_pb_e_kernel(
                 accum_out=negmean[c][:, j : j + 1],
             )
 
-        def sum_squares(c):
+        def sum_squares(c, j):
             if not exists(c):
                 return
-            sq[c] = stats.tile([P, PAIR], F32, name="sq")
-            for j in range(PAIR):
-                dropped = unread.tile([P, D], BF16)
-                nc.scalar.activation(
-                    out=dropped[:],
-                    in_=y_tiles[c][:, j, :],
-                    func=ACT.Square,
-                    bias=negmean[c][:, j : j + 1],
-                    scale=1.0,
-                    accum_out=sq[c][:, j : j + 1],
-                )
+            if j == 0:
+                sq[c] = stats.tile([P, PAIR], F32, name="sq")
+            dropped = unread.tile([P, D], BF16)
+            nc.scalar.activation(
+                out=dropped[:],
+                in_=y_tiles[c][:, j, :],
+                func=ACT.Square,
+                bias=negmean[c][:, j : j + 1],
+                scale=1.0,
+                accum_out=sq[c][:, j : j + 1],
+            )
 
         def root(c):
             if not exists(c):
                 return
-            std[c] = stats.tile([P, PAIR], F32, name="std")
+            rstd[c] = stats.tile([P, PAIR], F32, name="rstd")
             nc.scalar.activation(
-                out=std[c][:],
+                out=rstd[c][:],
                 in_=sq[c][:],
                 func=ACT.Abs_reciprocal_sqrt,
                 bias=eps[:, 0:1],
                 scale=1.0 / D,
             )
 
-        def centre_times_gain(c):
+        def centre_times_gain(c, j):
             if not exists(c):
                 return
-            o_c = o_pool.tile([P, PAIR, D], F32)
-            for j in range(PAIR):
-                nc.vector.scalar_tensor_tensor(
-                    out=o_c[:, j, :],
-                    in0=y_tiles[c][:, j, :],
-                    scalar=negmean[c][:, j : j + 1],
-                    in1=gain_psum[bank_of(c)][:],
-                    op0=ALU.add,
-                    op1=ALU.mult,
-                )
-            o_tiles[c] = o_c
+            if j == 0:
+                o_tiles[c] = o_pool.tile([P, PAIR, D], F32, name="o_c")
+            nc.vector.scalar_tensor_tensor(
+                out=o_tiles[c][:, j, :],
+                in0=y_tiles[c][:, j, :],
+                scalar=negmean[c][:, j : j + 1],
+                in1=gain_psum[bank_of(c)][:],
+                op0=ALU.add,
+                op1=ALU.mult,
+            )
 
         def finish(c, j):
             if not exists(c):
                 return
             last_adder = nc.vector if c == CHUNKS - 1 else nc.gpsimd
-            rstd = std[c]
             o_c = o_tiles[c]
             nc.vector.scalar_tensor_tensor(
                 out=o_c[:, j, :],
                 in0=o_c[:, j, :],
-                scalar=rstd[:, j : j + 1],
+                scalar=rstd[c][:, j : j + 1],
                 in1=bias_psum[bank_of(c)][:],
                 op0=ALU.mult,
                 op1=ALU.add,
@@ -304,41 +310,80 @@ def tile_moietransformerblock_pb_e_kernel(
                 out=out_rows[bank_of(c), :, first_tile_of(c) + j, :], in_=o_c[:, j, :]
             )
 
-        load_x(0)
-        load_weight_scales()
-        load_x(1)
-        load_x(2)
-        load_proto_w(0)
-        load_x(3)
-        load_proto_w(1)
-        load_x(4)
-        transpose(0)
-        regroup(0)
-        quantise(0)
-        transpose(1)
-        multiply(0)
-        regroup(1)
-        quantise(1)
-        transpose(2)
-        for c in range(CHUNKS + 1):
-            load_x(c + X_AHEAD)
+        def load_ahead(c):
+            for j in range(PAIR):
+                load_x(c + X_AHEAD, j)
+            if exists(c + X_AHEAD) and first_tile_of(c + X_AHEAD) == 0:
+                load_weight_scales(bank_of(c + X_AHEAD))
+                for h in range(HALVES):
+                    load_weight_words(bank_of(c + X_AHEAD), h)
             load_proto_w(c + PW_AHEAD)
+
+        load_x(0, 0)
+        load_weight_scales(0)
+        load_weight_words(0, 0)
+        load_x(0, 1)
+        load_weight_words(0, 1)
+        load_gain_and_bias()
+        for c in (1, 2):
+            for j in range(PAIR):
+                load_x(c, j)
+        load_proto_w(0)
+        for j in range(PAIR):
+            load_x(3, j)
+        load_proto_w(1)
+
+        transpose(0, 0)
+        regroup(0, 0, "scalar")
+        quantise(0, range(0, 1))
+        transpose(0, 1)
+        regroup(0, 1, "vector")
+        quantise(0, range(1, 2))
+        multiply(0, 0)
+        transpose(1, 0)
+        transpose(1, 1)
+        multiply(0, 1)
+        copy_and_sum(0, 0)
+        join_mean(0, 0)
+        regroup(1, 0, "vector")
+        regroup(1, 1, "vector")
+        quantise(1, range(PAIR))
+        sum_squares(0, 0)
+        transpose(2, 0)
+        transpose(2, 1)
+        spread_gain(0)
+        copy_and_sum(0, 1)
+        multiply(1, 0)
+        multiply(1, 1)
+        join_mean(0, 1)
+        spread_bias(0)
+        regroup(2, 0, "vector")
+        regroup(2, 1, "vector")
+        centre_times_gain(0, 0)
+        centre_times_gain(0, 1)
+        sum_squares(0, 1)
+        load_ahead(0)
+
+        for c in range(1, CHUNKS + 1):
+            load_ahead(c)
             root(c - 1)
-            spread_bias(c - 1)
+            if c > 1:
+                spread_bias(c - 1)
             finish(c - 1, 0)
-            if c > 0:
-                quantise(c + 2)
+            quantise(c + 1, range(PAIR))
             spread_gain(c)
-            copy_and_sum(c)
-            multiply(c + 1)
-            if c == 0:
-                regroup(2)
-                transpose(3)
-                quantise(2)
+            for j in range(PAIR):
+                transpose(c + 2, j)
+            for j in range(PAIR):
+                copy_and_sum(c, j)
+            for j in range(PAIR):
+                multiply(c + 1, j)
             join_mean(c, 0)
             finish(c - 1, 1)
             join_mean(c, 1)
-            regroup(c + 3)
-            transpose(c + 4)
-            centre_times_gain(c)
-            sum_squares(c)
+            for j in range(PAIR):
+                regroup(c + 2, j, "scalar")
+            for j in range(PAIR):
+                centre_times_gain(c, j)
+            for j in range(PAIR):
+                sum_squares(c, j)

@@ -66,7 +66,7 @@ def tile_moietransformerblock_pb_e_kernel(
     ):
         x_tiles, pw_tiles, xt_tiles, grouped_tiles, mx_rows, x_psum = {}, {}, {}, {}, {}, {}
         y_tiles, part_sum, negmean, sq, rstd, o_tiles = {}, {}, {}, {}, {}, {}
-        gain_psum, bias_psum, scaled = {}, {}, {}
+        gain_psum, bias_psum, scaled, added = {}, {}, {}, {}
 
         eps = consts.tile([P, 1], F32)
         nc.vector.memset(eps[:], LN_EPS)
@@ -79,6 +79,8 @@ def tile_moietransformerblock_pb_e_kernel(
 
         ident = consts.tile([P, P], F32)
         make_identity(nc, ident[:])
+        ident_bf16 = consts.tile([P, P], BF16)
+        make_identity(nc, ident_bf16[:])
 
         ones = consts.tile([P, P], BF16)
         nc.vector.memset(ones[:], 1.0)
@@ -218,6 +220,26 @@ def tile_moietransformerblock_pb_e_kernel(
             if exists(c) and first_tile_of(c) == 0:
                 bias_psum[bank_of(c)] = spread(c, bias_rows, "bias_wide")
 
+        def add_on_tensor(c, j, pool, tag):
+            for h in range(HALVES):
+                cols = slice(HALF * h, HALF * (h + 1))
+                total = pool.tile([P, HALF], F32, name=tag)
+                nc.tensor.matmul(
+                    out=total[:],
+                    lhsT=ident_bf16[:],
+                    rhs=pw_tiles[c][:, j, cols],
+                    start=True,
+                    stop=False,
+                )
+                nc.tensor.matmul(
+                    out=total[:],
+                    lhsT=ones[:],
+                    rhs=bias_rows[:, bank_of(c), cols],
+                    start=False,
+                    stop=True,
+                )
+                added[c, j, h] = total
+
         def copy_and_sum(c, j):
             if not exists(c):
                 return
@@ -263,13 +285,14 @@ def tile_moietransformerblock_pb_e_kernel(
                 accum_out=sq[c][:, j : j + 1],
             )
 
-        def root(c):
+        def root(c, tiles):
             if not exists(c):
                 return
-            rstd[c] = stats.tile([P, PAIR], F32, name="rstd")
+            if tiles.start == 0:
+                rstd[c] = stats.tile([P, PAIR], F32, name="rstd")
             nc.scalar.activation(
-                out=rstd[c][:],
-                in_=sq[c][:],
+                out=rstd[c][:, tiles.start : tiles.stop],
+                in_=sq[c][:, tiles.start : tiles.stop],
                 func=ACT.Abs_reciprocal_sqrt,
                 bias=eps[:, 0:1],
                 scale=1.0 / D,
@@ -292,8 +315,22 @@ def tile_moietransformerblock_pb_e_kernel(
         def finish(c, j):
             if not exists(c):
                 return
-            last_adder = nc.vector if c == CHUNKS - 1 else nc.gpsimd
             o_c = o_tiles[c]
+            if (c, j, 0) in added:
+                for h in range(HALVES):
+                    cols = slice(HALF * h, HALF * (h + 1))
+                    nc.vector.scalar_tensor_tensor(
+                        out=o_c[:, j, cols],
+                        in0=o_c[:, j, cols],
+                        scalar=rstd[c][:, j : j + 1],
+                        in1=added[c, j, h][:],
+                        op0=ALU.mult,
+                        op1=ALU.add,
+                    )
+                    nc.sync.dma_start(
+                        out=out_rows[bank_of(c), :, first_tile_of(c) + j, cols], in_=o_c[:, j, cols]
+                    )
+                return
             nc.vector.scalar_tensor_tensor(
                 out=o_c[:, j, :],
                 in0=o_c[:, j, :],
@@ -302,8 +339,7 @@ def tile_moietransformerblock_pb_e_kernel(
                 op0=ALU.mult,
                 op1=ALU.add,
             )
-            adder = last_adder if j == PAIR - 1 else nc.gpsimd
-            adder.tensor_tensor(
+            nc.gpsimd.tensor_tensor(
                 out=o_c[:, j, :], in0=o_c[:, j, :], in1=pw_tiles[c][:, j, :], op=ALU.add
             )
             nc.sync.dma_start(
@@ -366,7 +402,8 @@ def tile_moietransformerblock_pb_e_kernel(
 
         for c in range(1, CHUNKS + 1):
             load_ahead(c)
-            root(c - 1)
+            if c < CHUNKS:
+                root(c - 1, range(PAIR))
             if c > 1:
                 spread_bias(c - 1)
             finish(c - 1, 0)
@@ -378,6 +415,10 @@ def tile_moietransformerblock_pb_e_kernel(
                 copy_and_sum(c, j)
             for j in range(PAIR):
                 multiply(c + 1, j)
+            if c == CHUNKS - 1:
+                add_on_tensor(c - 1, 1, xt_pool, "xt")
+                for j in range(PAIR):
+                    add_on_tensor(c, j, acc_pool, "acc")
             join_mean(c, 0)
             finish(c - 1, 1)
             join_mean(c, 1)
@@ -387,3 +428,5 @@ def tile_moietransformerblock_pb_e_kernel(
                 centre_times_gain(c, j)
             for j in range(PAIR):
                 sum_squares(c, j)
+                if c == CHUNKS - 1:
+                    root(c, range(j, j + 1))

@@ -68,6 +68,8 @@ def tile_moietransformerblock_pb_e_kernel(
         y_tiles, part_sum, negmean, sq, rstd, o_tiles = {}, {}, {}, {}, {}, {}
         gain_psum, bias_psum, scaled, added = {}, {}, {}, {}
 
+        zeros = consts.tile([P, HALF], BF16)
+        nc.vector.memset(zeros[:].bitcast(I32), 0)
         eps = consts.tile([P, 1], F32)
         nc.vector.memset(eps[:], LN_EPS)
         w_scales = consts.tile([P, BANKS * PASSES, D], U8, align_bytes=64)
@@ -133,6 +135,13 @@ def tile_moietransformerblock_pb_e_kernel(
             pw_c = pw_pool.tile([P, PAIR, D], BF16)
             nc.sync.dma_start(out=pw_c[:], in_=pw_rows[bank_of(c), :, first : first + PAIR, :])
             pw_tiles[c] = pw_c
+
+        def warm_up(count):
+            unused = acc_pool.tile([P, HALF], F32, name="acc")
+            for i in range(count):
+                nc.tensor.matmul(
+                    out=unused[:], lhsT=zeros[:, 0:P], rhs=zeros[:], start=True, stop=True
+                )
 
         def transpose(c, j):
             if not exists(c):
@@ -369,7 +378,9 @@ def tile_moietransformerblock_pb_e_kernel(
             load_x(3, j)
         load_proto_w(1)
 
+        warm_up(4)
         transpose(0, 0)
+        warm_up(2)
         regroup(0, 0, "scalar")
         quantise(0, range(0, 1))
         transpose(0, 1)
@@ -422,8 +433,8 @@ def tile_moietransformerblock_pb_e_kernel(
             join_mean(c, 0)
             finish(c - 1, 1)
             join_mean(c, 1)
-            for j in range(PAIR):
-                regroup(c + 2, j, "scalar")
+            regroup(c + 2, 0, "scalar")
+            regroup(c + 2, 1, "vector" if c % 2 == 0 else "scalar")
             for j in range(PAIR):
                 centre_times_gain(c, j)
             for j in range(PAIR):

@@ -249,19 +249,18 @@ def tile_moietransformerblock_pb_e_kernel(
                 )
                 added[c, j, h] = total
 
-        def copy_and_sum(c, j):
+        def copy_and_sum(c, j, h):
             if not exists(c):
                 return
-            if j == 0:
+            if j == 0 and h == 0:
                 y_tiles[c] = y_pool.tile([P, PAIR, D], F32, name="y_c")
                 part_sum[c] = stats.tile([P, PAIR, HALVES], F32, name="sums")
-            for h in range(HALVES):
-                nc.scalar.activation(
-                    out=y_tiles[c][:, j, HALF * h : HALF * (h + 1)],
-                    in_=x_psum[c, j, h][:],
-                    func=ACT.Copy,
-                    accum_out=part_sum[c][:, j, h : h + 1],
-                )
+            nc.scalar.activation(
+                out=y_tiles[c][:, j, HALF * h : HALF * (h + 1)],
+                in_=x_psum[c, j, h][:],
+                func=ACT.Copy,
+                accum_out=part_sum[c][:, j, h : h + 1],
+            )
 
         def join_mean(c, j):
             if not exists(c):
@@ -390,7 +389,8 @@ def tile_moietransformerblock_pb_e_kernel(
         transpose(1, 0)
         transpose(1, 1)
         multiply(0, 1)
-        copy_and_sum(0, 0)
+        copy_and_sum(0, 0, 0)
+        copy_and_sum(0, 0, 1)
         join_mean(0, 0)
         regroup(1, 0, "vector")
         regroup(1, 1, "vector")
@@ -399,7 +399,8 @@ def tile_moietransformerblock_pb_e_kernel(
         transpose(2, 0)
         transpose(2, 1)
         spread_gain(0)
-        copy_and_sum(0, 1)
+        copy_and_sum(0, 1, 0)
+        copy_and_sum(0, 1, 1)
         multiply(1, 0)
         multiply(1, 1)
         join_mean(0, 1)
@@ -414,7 +415,7 @@ def tile_moietransformerblock_pb_e_kernel(
         for c in range(1, CHUNKS + 1):
             load_ahead(c)
             if c < CHUNKS:
-                root(c - 1, range(PAIR))
+                root(c - 1, range(0, 1))
             if c > 1:
                 spread_bias(c - 1)
             finish(c - 1, 0)
@@ -422,8 +423,12 @@ def tile_moietransformerblock_pb_e_kernel(
             spread_gain(c)
             for j in range(PAIR):
                 transpose(c + 2, j)
-            for j in range(PAIR):
-                copy_and_sum(c, j)
+            copy_and_sum(c, 0, 0)
+            if c < CHUNKS:
+                root(c - 1, range(1, 2))
+            copy_and_sum(c, 0, 1)
+            for h in range(HALVES):
+                copy_and_sum(c, 1, h)
             for j in range(PAIR):
                 multiply(c + 1, j)
             if c == CHUNKS - 1:

@@ -268,13 +268,11 @@ def tile_moietransformerblock_pb_e_kernel(
             if j == 0:
                 scaled[c] = stats.tile([P, PAIR, HALVES], F32, name="scaled")
                 negmean[c] = stats.tile([P, PAIR], F32, name="negmean")
-            nc.vector.tensor_scalar(
+            nc.scalar.activation(
                 out=scaled[c][:, j, :],
-                in0=part_sum[c][:, j, :],
-                scalar1=-1.0 / D,
-                scalar2=None,
-                op0=ALU.mult,
-                op1=ALU.add,
+                in_=part_sum[c][:, j, :],
+                func=ACT.Copy,
+                scale=-1.0 / D,
                 accum_out=negmean[c][:, j : j + 1],
             )
 
@@ -427,18 +425,18 @@ def tile_moietransformerblock_pb_e_kernel(
             if c < CHUNKS:
                 root(c - 1, range(1, 2))
             copy_and_sum(c, 0, 1)
-            for h in range(HALVES):
-                copy_and_sum(c, 1, h)
+            copy_and_sum(c, 1, 0)
+            join_mean(c, 0)
+            copy_and_sum(c, 1, 1)
             for j in range(PAIR):
                 multiply(c + 1, j)
             if c == CHUNKS - 1:
                 add_on_tensor(c - 1, 1, xt_pool, "xt")
                 for j in range(PAIR):
                     add_on_tensor(c, j, acc_pool, "acc")
-            join_mean(c, 0)
             finish(c - 1, 1)
-            join_mean(c, 1)
             regroup(c + 2, 0, "scalar")
+            join_mean(c, 1)
             regroup(c + 2, 1, "vector" if c % 2 == 0 else "scalar")
             for j in range(PAIR):
                 centre_times_gain(c, j)

@@ -29,6 +29,8 @@ CHUNKS = BANKS * CHUNKS_PER_BANK
 X_AHEAD = 4
 PW_AHEAD = 2
 
+LAST_TILE = (CHUNKS - 1, PAIR - 1)
+
 FLOPS = 2 * BANKS * ROWS * K * D
 
 
@@ -59,6 +61,7 @@ def tile_moietransformerblock_pb_e_kernel(
         tc.tile_pool(name="o_pool", bufs=4) as o_pool,
         tc.tile_pool(name="unread", bufs=2) as unread,
         tc.tile_pool(name="stats", bufs=3) as stats,
+        tc.tile_pool(name="helper", bufs=1) as helper,
         tc.psum_pool(name="xt_pool", bufs=PAIR) as xt_pool,
         tc.psum_pool(name="spread_pool", bufs=1) as spread_pool,
         tc.psum_pool(name="acc_pool", bufs=PAIR * HALVES) as acc_pool,
@@ -91,6 +94,7 @@ def tile_moietransformerblock_pb_e_kernel(
         bias_rows = consts.tile([P, BANKS, D], BF16)
         nc.vector.memset(bias_rows[:].bitcast(I32), 0)
         nc.vector.memset(w_scales[:, PASSES:, :].bitcast(I32), 0)
+        gain_sbuf = consts.tile([P, HALF], BF16)
 
         def load_x(c, j):
             if not exists(c):
@@ -309,13 +313,31 @@ def tile_moietransformerblock_pb_e_kernel(
                 return
             if j == 0:
                 o_tiles[c] = o_pool.tile([P, PAIR, D], F32, name="o_c")
+            width = HALF if (c, j) == LAST_TILE else D
             nc.vector.scalar_tensor_tensor(
-                out=o_tiles[c][:, j, :],
-                in0=y_tiles[c][:, j, :],
+                out=o_tiles[c][:, j, 0:width],
+                in0=y_tiles[c][:, j, 0:width],
                 scalar=negmean[c][:, j : j + 1],
-                in1=gain_psum[bank_of(c)][:],
+                in1=gain_psum[bank_of(c)][:, 0:width],
                 op0=ALU.add,
                 op1=ALU.mult,
+            )
+
+        def copy_gain_for_gpsimd():
+            nc.vector.tensor_copy(out=gain_sbuf[:], in_=gain_psum[BANKS - 1][:, HALF:])
+
+        def centre_times_gain_on_gpsimd(c, j):
+            centred = helper.tile([P, HALF], F32)
+            nc.gpsimd.tensor_scalar(
+                out=centred[:],
+                in0=y_tiles[c][:, j, HALF:],
+                scalar1=1.0,
+                scalar2=negmean[c][:, j : j + 1],
+                op0=ALU.mult,
+                op1=ALU.add,
+            )
+            nc.gpsimd.tensor_tensor(
+                out=o_tiles[c][:, j, HALF:], in0=centred[:], in1=gain_sbuf[:], op=ALU.mult
             )
 
         def finish(c, j):
@@ -440,6 +462,10 @@ def tile_moietransformerblock_pb_e_kernel(
             regroup(c + 2, 1, "vector" if c % 2 == 0 else "scalar")
             for j in range(PAIR):
                 centre_times_gain(c, j)
+            if c == CHUNKS - 3:
+                copy_gain_for_gpsimd()
+            if c == CHUNKS - 1:
+                centre_times_gain_on_gpsimd(c, PAIR - 1)
             for j in range(PAIR):
                 sum_squares(c, j)
                 if c == CHUNKS - 1:

@@ -29,7 +29,8 @@ CHUNKS = BANKS * CHUNKS_PER_BANK
 X_AHEAD = 4
 PW_AHEAD = 2
 
-LAST_TILE = (CHUNKS - 1, PAIR - 1)
+SUMS_ON_TENSOR = ((CHUNKS - 3, 1), (CHUNKS - 2, 0), (CHUNKS - 2, 1), (CHUNKS - 1, 0), (CHUNKS - 1, 1))
+HALVED = SUMS_ON_TENSOR[2:]
 
 FLOPS = 2 * BANKS * ROWS * K * D
 
@@ -61,7 +62,7 @@ def tile_moietransformerblock_pb_e_kernel(
         tc.tile_pool(name="o_pool", bufs=4) as o_pool,
         tc.tile_pool(name="unread", bufs=2) as unread,
         tc.tile_pool(name="stats", bufs=3) as stats,
-        tc.tile_pool(name="helper", bufs=1) as helper,
+        tc.tile_pool(name="helper", bufs=2) as helper,
         tc.psum_pool(name="xt_pool", bufs=PAIR) as xt_pool,
         tc.psum_pool(name="spread_pool", bufs=1) as spread_pool,
         tc.psum_pool(name="acc_pool", bufs=PAIR * HALVES) as acc_pool,
@@ -313,7 +314,7 @@ def tile_moietransformerblock_pb_e_kernel(
                 return
             if j == 0:
                 o_tiles[c] = o_pool.tile([P, PAIR, D], F32, name="o_c")
-            width = HALF if (c, j) == LAST_TILE else D
+            width = HALF if (c, j) in HALVED else D
             nc.vector.scalar_tensor_tensor(
                 out=o_tiles[c][:, j, 0:width],
                 in0=y_tiles[c][:, j, 0:width],
@@ -453,19 +454,24 @@ def tile_moietransformerblock_pb_e_kernel(
             for j in range(PAIR):
                 multiply(c + 1, j)
             if c == CHUNKS - 1:
-                add_on_tensor(c - 1, 1, xt_pool, "xt")
-                for j in range(PAIR):
-                    add_on_tensor(c, j, acc_pool, "acc")
+                add_on_tensor(c - 1, 1, acc_pool, "acc")
+                add_on_tensor(c, 0, xt_pool, "xt")
+                add_on_tensor(c, 1, acc_pool, "acc")
             finish(c - 1, 1)
+            if c == CHUNKS - 2:
+                add_on_tensor(c, 0, xt_pool, "xt")
             regroup(c + 2, 0, "scalar")
             join_mean(c, 1)
-            regroup(c + 2, 1, "vector" if c % 2 == 0 else "scalar")
+            regroup(c + 2, 1, "vector" if c % 2 == 0 or c == CHUNKS - 3 else "scalar")
+            if c == CHUNKS - 3:
+                add_on_tensor(c, 1, xt_pool, "xt")
             for j in range(PAIR):
                 centre_times_gain(c, j)
             if c == CHUNKS - 3:
                 copy_gain_for_gpsimd()
-            if c == CHUNKS - 1:
-                centre_times_gain_on_gpsimd(c, PAIR - 1)
+            for j in range(PAIR):
+                if (c, j) in HALVED:
+                    centre_times_gain_on_gpsimd(c, j)
             for j in range(PAIR):
                 sum_squares(c, j)
                 if c == CHUNKS - 1:

@@ -30,7 +30,7 @@ X_AHEAD = 4
 PW_AHEAD = 2
 
 SUMS_ON_TENSOR = ((CHUNKS - 3, 1), (CHUNKS - 2, 0), (CHUNKS - 2, 1), (CHUNKS - 1, 0), (CHUNKS - 1, 1))
-HALVED = SUMS_ON_TENSOR[2:]
+HALVED = ((0, 0), (0, 1)) + SUMS_ON_TENSOR[2:]
 
 FLOPS = 2 * BANKS * ROWS * K * D
 
@@ -78,6 +78,8 @@ def tile_moietransformerblock_pb_e_kernel(
         nc.vector.memset(eps[:], LN_EPS)
         w_scales = consts.tile([P, BANKS * PASSES, D], U8, align_bytes=64)
         nc.vector.memset(w_scales[:, 0:PASSES, :].bitcast(I32), 0)
+        gain_rows = consts.tile([P, BANKS, D], BF16)
+        nc.vector.memset(gain_rows[:, 0, :].bitcast(I32), 0)
         w_words = consts.tile([P, BANKS * PASSES, 2 * D], U8, align_bytes=64)
 
         first_sqrt = consts.tile([P, 1], F32)
@@ -90,12 +92,11 @@ def tile_moietransformerblock_pb_e_kernel(
 
         ones = consts.tile([P, P], BF16)
         nc.vector.memset(ones[:], 1.0)
-        gain_rows = consts.tile([P, BANKS, D], BF16)
-        nc.vector.memset(gain_rows[:].bitcast(I32), 0)
+        nc.vector.memset(gain_rows[:, 1:, :].bitcast(I32), 0)
         bias_rows = consts.tile([P, BANKS, D], BF16)
         nc.vector.memset(bias_rows[:].bitcast(I32), 0)
         nc.vector.memset(w_scales[:, PASSES:, :].bitcast(I32), 0)
-        gain_sbuf = consts.tile([P, HALF], BF16)
+        gain_sbuf = consts.tile([P, BANKS, HALF], BF16)
 
         def load_x(c, j):
             if not exists(c):
@@ -123,10 +124,13 @@ def tile_moietransformerblock_pb_e_kernel(
                     in_=scale_rows[passes, r:16:4, :].rearrange("g c n -> c g n"),
                 )
 
+        def load_first_gain():
+            nc.sync.dma_start(out=gain_rows[0:1, 0, :], in_=pln_g[0:1, :])
+
         def load_gain_and_bias():
             nc.sync.dma_start(
-                out=gain_rows[0:1, :, :].rearrange("o n d -> o (n d)"),
-                in_=pln_g.rearrange("n d -> (n d)").unsqueeze(0),
+                out=gain_rows[0:1, 1:, :].rearrange("o n d -> o (n d)"),
+                in_=pln_g[1:, :].rearrange("n d -> (n d)").unsqueeze(0),
             )
             nc.sync.dma_start(
                 out=bias_rows[0:1, :, :].rearrange("o n d -> o (n d)"),
@@ -324,8 +328,8 @@ def tile_moietransformerblock_pb_e_kernel(
                 op1=ALU.mult,
             )
 
-        def copy_gain_for_gpsimd():
-            nc.vector.tensor_copy(out=gain_sbuf[:], in_=gain_psum[BANKS - 1][:, HALF:])
+        def copy_gain_for_gpsimd(n):
+            nc.vector.tensor_copy(out=gain_sbuf[:, n, :], in_=gain_psum[n][:, HALF:])
 
         def centre_times_gain_on_gpsimd(c, j):
             centred = helper.tile([P, HALF], F32)
@@ -338,7 +342,10 @@ def tile_moietransformerblock_pb_e_kernel(
                 op1=ALU.add,
             )
             nc.gpsimd.tensor_tensor(
-                out=o_tiles[c][:, j, HALF:], in0=centred[:], in1=gain_sbuf[:], op=ALU.mult
+                out=o_tiles[c][:, j, HALF:],
+                in0=centred[:],
+                in1=gain_sbuf[:, bank_of(c), :],
+                op=ALU.mult,
             )
 
         def finish(c, j):
@@ -386,6 +393,7 @@ def tile_moietransformerblock_pb_e_kernel(
 
         load_x(0, 0)
         load_weight_scales(0)
+        load_first_gain()
         load_weight_words(0, 0)
         load_x(0, 1)
         load_weight_words(0, 1)
@@ -400,12 +408,13 @@ def tile_moietransformerblock_pb_e_kernel(
 
         warm_up(4)
         transpose(0, 0)
-        warm_up(2)
+        spread_gain(0)
         regroup(0, 0, "scalar")
         quantise(0, range(0, 1))
         transpose(0, 1)
         regroup(0, 1, "vector")
         quantise(0, range(1, 2))
+        copy_gain_for_gpsimd(0)
         multiply(0, 0)
         transpose(1, 0)
         transpose(1, 1)
@@ -416,10 +425,11 @@ def tile_moietransformerblock_pb_e_kernel(
         regroup(1, 0, "vector")
         regroup(1, 1, "vector")
         quantise(1, range(PAIR))
+        centre_times_gain(0, 0)
+        centre_times_gain_on_gpsimd(0, 0)
         sum_squares(0, 0)
         transpose(2, 0)
         transpose(2, 1)
-        spread_gain(0)
         copy_and_sum(0, 1, 0)
         copy_and_sum(0, 1, 1)
         multiply(1, 0)
@@ -428,8 +438,8 @@ def tile_moietransformerblock_pb_e_kernel(
         spread_bias(0)
         regroup(2, 0, "vector")
         regroup(2, 1, "vector")
-        centre_times_gain(0, 0)
         centre_times_gain(0, 1)
+        centre_times_gain_on_gpsimd(0, 1)
         sum_squares(0, 1)
         load_ahead(0)
 
@@ -468,7 +478,7 @@ def tile_moietransformerblock_pb_e_kernel(
             for j in range(PAIR):
                 centre_times_gain(c, j)
             if c == CHUNKS - 3:
-                copy_gain_for_gpsimd()
+                copy_gain_for_gpsimd(BANKS - 1)
             for j in range(PAIR):
                 if (c, j) in HALVED:
                     centre_times_gain_on_gpsimd(c, j)

@@ -78,8 +78,8 @@ def tile_moietransformerblock_pb_e_kernel(
         nc.vector.memset(eps[:], LN_EPS)
         w_scales = consts.tile([P, BANKS * PASSES, D], U8, align_bytes=64)
         nc.vector.memset(w_scales[:, 0:PASSES, :].bitcast(I32), 0)
-        gain_rows = consts.tile([P, BANKS, D], BF16)
-        nc.vector.memset(gain_rows[:, 0, :].bitcast(I32), 0)
+        gain_row = consts.tile([P, D], BF16)
+        nc.vector.memset(gain_row[:].bitcast(I32), 0)
         w_words = consts.tile([P, BANKS * PASSES, 2 * D], U8, align_bytes=64)
 
         first_sqrt = consts.tile([P, 1], F32)
@@ -92,10 +92,8 @@ def tile_moietransformerblock_pb_e_kernel(
 
         ones = consts.tile([P, P], BF16)
         nc.vector.memset(ones[:], 1.0)
-        nc.vector.memset(gain_rows[:, 1:, :].bitcast(I32), 0)
-        bias_rows = consts.tile([P, BANKS, D], BF16)
-        nc.vector.memset(bias_rows[:].bitcast(I32), 0)
-        nc.vector.memset(w_scales[:, PASSES:, :].bitcast(I32), 0)
+        bias_row = consts.tile([P, D], BF16)
+        nc.vector.memset(bias_row[:].bitcast(I32), 0)
         gain_sbuf = consts.tile([P, BANKS, HALF], BF16)
 
         def load_x(c, j):
@@ -124,18 +122,11 @@ def tile_moietransformerblock_pb_e_kernel(
                     in_=scale_rows[passes, r:16:4, :].rearrange("g c n -> c g n"),
                 )
 
-        def load_first_gain():
-            nc.sync.dma_start(out=gain_rows[0:1, 0, :], in_=pln_g[0:1, :])
+        def load_gain(n):
+            nc.sync.dma_start(out=gain_row[0:1, :], in_=pln_g[n : n + 1, :])
 
-        def load_gain_and_bias():
-            nc.sync.dma_start(
-                out=gain_rows[0:1, 1:, :].rearrange("o n d -> o (n d)"),
-                in_=pln_g[1:, :].rearrange("n d -> (n d)").unsqueeze(0),
-            )
-            nc.sync.dma_start(
-                out=bias_rows[0:1, :, :].rearrange("o n d -> o (n d)"),
-                in_=pln_b.rearrange("n d -> (n d)").unsqueeze(0),
-            )
+        def load_bias(n):
+            nc.sync.dma_start(out=bias_row[0:1, :], in_=pln_b[n : n + 1, :])
 
         def load_proto_w(c):
             if not exists(c):
@@ -224,7 +215,7 @@ def tile_moietransformerblock_pb_e_kernel(
                 nc.tensor.matmul(
                     out=wide[:, cols],
                     lhsT=ones[:],
-                    rhs=rows_of_banks[:, bank_of(c), cols],
+                    rhs=rows_of_banks[:, cols],
                     start=True,
                     stop=True,
                 )
@@ -232,11 +223,11 @@ def tile_moietransformerblock_pb_e_kernel(
 
         def spread_gain(c):
             if exists(c) and first_tile_of(c) == 0:
-                gain_psum[bank_of(c)] = spread(c, gain_rows, "gain_wide")
+                gain_psum[bank_of(c)] = spread(c, gain_row, "gain_wide")
 
         def spread_bias(c):
             if exists(c) and first_tile_of(c) == 0:
-                bias_psum[bank_of(c)] = spread(c, bias_rows, "bias_wide")
+                bias_psum[bank_of(c)] = spread(c, bias_row, "bias_wide")
 
         def add_on_tensor(c, j, pool, tag):
             for h in range(HALVES):
@@ -252,7 +243,7 @@ def tile_moietransformerblock_pb_e_kernel(
                 nc.tensor.matmul(
                     out=total[:],
                     lhsT=ones[:],
-                    rhs=bias_rows[:, bank_of(c), cols],
+                    rhs=bias_row[:, cols],
                     start=False,
                     stop=True,
                 )
@@ -390,14 +381,18 @@ def tile_moietransformerblock_pb_e_kernel(
                 for h in range(HALVES):
                     load_weight_words(bank_of(c + X_AHEAD), h)
             load_proto_w(c + PW_AHEAD)
+            if c in (0, 5):
+                load_gain(1 + (0, 5).index(c))
+            if c in (2, 6):
+                load_bias(1 + (2, 6).index(c))
 
         load_x(0, 0)
         load_weight_scales(0)
-        load_first_gain()
+        load_gain(0)
         load_weight_words(0, 0)
         load_x(0, 1)
         load_weight_words(0, 1)
-        load_gain_and_bias()
+        load_bias(0)
         for c in (1, 2):
             for j in range(PAIR):
                 load_x(c, j)
@@ -412,7 +407,7 @@ def tile_moietransformerblock_pb_e_kernel(
         regroup(0, 0, "scalar")
         quantise(0, range(0, 1))
         transpose(0, 1)
-        regroup(0, 1, "vector")
+        regroup(0, 1, "scalar")
         quantise(0, range(1, 2))
         copy_gain_for_gpsimd(0)
         multiply(0, 0)
@@ -425,6 +420,7 @@ def tile_moietransformerblock_pb_e_kernel(
         regroup(1, 0, "vector")
         regroup(1, 1, "vector")
         quantise(1, range(PAIR))
+        nc.vector.memset(w_scales[:, PASSES:, :].bitcast(I32), 0)
         centre_times_gain(0, 0)
         centre_times_gain_on_gpsimd(0, 0)
         sum_squares(0, 0)

import concourse.mybir as mybir
from concourse.masks import make_identity

F32 = mybir.dt.float32
BF16 = mybir.dt.bfloat16
I32 = mybir.dt.int32
U32 = mybir.dt.uint32
U8 = mybir.dt.uint8
FP8X4 = mybir.dt.float8_e4m3fn_x4
FP4X4 = mybir.dt.float4_e2m1fn_x4
ALU = mybir.AluOpType
ACT = mybir.ActivationFunctionType

BANKS = 3
ROWS = 1024
K = 1024
D = 1024
LN_EPS = 1e-5

P = 128
K_PASS = 4 * P
PASSES = K // K_PASS
HALF = 512
HALVES = D // HALF
ROW_TILES = ROWS // P
PAIR = 2
CHUNKS_PER_BANK = ROW_TILES // PAIR
CHUNKS = BANKS * CHUNKS_PER_BANK
X_AHEAD = 4
PW_AHEAD = 2

SUMS_ON_TENSOR = ((CHUNKS - 3, 1), (CHUNKS - 2, 0), (CHUNKS - 2, 1), (CHUNKS - 1, 0), (CHUNKS - 1, 1))
HALVED = ((0, 0), (0, 1)) + SUMS_ON_TENSOR[2:]

FLOPS = 2 * BANKS * ROWS * K * D


def tile_moietransformerblock_pb_e_kernel(
    tc, in_proto, pt_w_words, pt_w_scales, pln_g, pln_b, proto_w, out
):
    nc = tc.nc

    x_rows = in_proto.rearrange("n (p t) k -> n p t k", t=ROW_TILES)
    pw_rows = proto_w.rearrange("n (p t) d -> n p t d", t=ROW_TILES)
    out_rows = out.rearrange("n (p t) d -> n p t d", t=ROW_TILES)

    def bank_of(c):
        return c // CHUNKS_PER_BANK

    def first_tile_of(c):
        return PAIR * (c % CHUNKS_PER_BANK)

    def exists(c):
        return 0 <= c < CHUNKS

    with (
        tc.tile_pool(name="consts", bufs=1) as consts,
        tc.tile_pool(name="x_pool", bufs=X_AHEAD + 1) as x_pool,
        tc.tile_pool(name="pw_pool", bufs=PW_AHEAD + 4) as pw_pool,
        tc.tile_pool(name="quant", bufs=3) as quant,
        tc.tile_pool(name="y_pool", bufs=3) as y_pool,
        tc.tile_pool(name="o_pool", bufs=4) as o_pool,
        tc.tile_pool(name="unread", bufs=2) as unread,
        tc.tile_pool(name="stats", bufs=3) as stats,
        tc.tile_pool(name="helper", bufs=2) as helper,
        tc.psum_pool(name="xt_pool", bufs=PAIR) as xt_pool,
        tc.psum_pool(name="spread_pool", bufs=1) as spread_pool,
        tc.psum_pool(name="acc_pool", bufs=PAIR * HALVES) as acc_pool,
        tc.manual_schedule(),
    ):
        x_tiles, pw_tiles, xt_tiles, grouped_tiles, mx_rows, x_psum = {}, {}, {}, {}, {}, {}
        y_tiles, part_sum, negmean, sq, rstd, o_tiles = {}, {}, {}, {}, {}, {}
        gain_psum, bias_psum, scaled, added = {}, {}, {}, {}

        zeros = consts.tile([P, HALF], BF16)
        nc.vector.memset(zeros[:].bitcast(I32), 0)
        eps = consts.tile([P, 1], F32)
        nc.vector.memset(eps[:], LN_EPS)
        w_scales = consts.tile([P, BANKS * PASSES, D], U8, align_bytes=64)
        nc.vector.memset(w_scales[:, 0:PASSES, :].bitcast(I32), 0)
        gain_row = consts.tile([P, D], BF16)
        nc.vector.memset(gain_row[:].bitcast(I32), 0)
        w_words = consts.tile([P, BANKS * PASSES, 2 * D], U8, align_bytes=64)

        first_sqrt = consts.tile([P, 1], F32)
        nc.scalar.activation(out=first_sqrt[:], in_=eps[:], func=ACT.Abs_reciprocal_sqrt)

        ident = consts.tile([P, P], F32)
        make_identity(nc, ident[:])
        ident_bf16 = consts.tile([P, P], BF16)
        make_identity(nc, ident_bf16[:])

        ones = consts.tile([P, P], BF16)
        nc.vector.memset(ones[:], 1.0)
        bias_row = consts.tile([P, D], BF16)
        nc.vector.memset(bias_row[:].bitcast(I32), 0)
        gain_sbuf = consts.tile([P, BANKS, HALF], BF16)

        def load_x(c, j):
            if not exists(c):
                return
            if j == 0:
                x_tiles[c] = x_pool.tile([P, PAIR, K], BF16, name="x_c")
            nc.sync.dma_start(
                out=x_tiles[c][:, j, :], in_=x_rows[bank_of(c), :, first_tile_of(c) + j, :]
            )

        def load_weight_words(n, h):
            passes = slice(PASSES * n, PASSES * (n + 1))
            cols = slice(2 * HALF * h, 2 * HALF * (h + 1))
            nc.sync.dma_start(
                out=w_words[:, passes, cols].bitcast(I32),
                in_=pt_w_words[passes, :, cols].bitcast(I32).rearrange("g p n -> p g n"),
            )

        def load_weight_scales(n):
            passes = slice(PASSES * n, PASSES * (n + 1))
            scale_rows = pt_w_scales.bitcast(I32)
            for r in range(4):
                nc.sync.dma_start(
                    out=w_scales[r:P:32, passes, :].bitcast(I32),
                    in_=scale_rows[passes, r:16:4, :].rearrange("g c n -> c g n"),
                )

        def load_gain(n):
            nc.sync.dma_start(out=gain_row[0:1, :], in_=pln_g[n : n + 1, :])

        def load_bias(n):
            nc.sync.dma_start(out=bias_row[0:1, :], in_=pln_b[n : n + 1, :])

        def load_proto_w(c):
            if not exists(c):
                return
            first = first_tile_of(c)
            pw_c = pw_pool.tile([P, PAIR, D], BF16)
            nc.sync.dma_start(out=pw_c[:], in_=pw_rows[bank_of(c), :, first : first + PAIR, :])
            pw_tiles[c] = pw_c

        def warm_up(count):
            unused = acc_pool.tile([P, HALF], F32, name="acc")
            for i in range(count):
                nc.tensor.matmul(
                    out=unused[:], lhsT=zeros[:, 0:P], rhs=zeros[:], start=True, stop=True
                )

        def transpose(c, j):
            if not exists(c):
                return
            x_words = x_tiles[c][:, j, :].bitcast(F32)
            xt = xt_pool.tile([P, PASSES, 2, P], F32)
            for s in range(PASSES):
                for u in range(2):
                    nc.tensor.transpose(
                        xt[:, s, u, :],
                        x_words[:, 2 * P * s + u : 2 * P * (s + 1) : 2],
                        ident[:],
                    )
            xt_tiles[c, j] = xt

        def regroup(c, j, engine):
            if not exists(c):
                return
            if j == 0:
                grouped_tiles[c] = quant.tile([P, PAIR, K], BF16, align_bytes=64, name="grouped")
            side_by_side = (
                grouped_tiles[c][:, j, :]
                .bitcast(F32)
                .rearrange("p (s r u) -> p s r u", s=PASSES, u=2)
            )
            transposed = xt_tiles[c, j][:].rearrange("p s u r -> p s r u")
            if engine == "scalar":
                nc.scalar.copy(out=side_by_side, in_=transposed)
            else:
                nc.vector.tensor_copy(out=side_by_side, in_=transposed)

        def quantise(c, tiles):
            if not exists(c):
                return
            if tiles.start == 0:
                codes = quant.tile([P, PAIR * PASSES * P], U32, align_bytes=64)
                scales = quant.tile([P, PAIR * PASSES * P], U8, align_bytes=64)
                mx_rows[c] = (codes, scales)
            codes, scales = mx_rows[c]
            cols = slice(tiles.start * PASSES * P, tiles.stop * PASSES * P)
            nc.vector.quantize_mx(
                out=codes[:, cols].bitcast(FP8X4),
                scales=scales[:, cols],
                in_=grouped_tiles[c][:, tiles.start : tiles.stop, :].rearrange("p j k -> p (j k)"),
            )

        def multiply(c, j):
            if not exists(c):
                return
            codes, scales = mx_rows[c]
            for h in range(HALVES):
                acc = acc_pool.tile([P, HALF], F32)
                for s in range(PASSES):
                    rows = slice((j * PASSES + s) * P, (j * PASSES + s + 1) * P)
                    g = bank_of(c) * PASSES + s
                    nc.tensor.matmul_mx(
                        out=acc[:],
                        lhsT=codes[:, rows].bitcast(FP8X4),
                        lhsT_scale=scales[:, rows],
                        rhs=w_words[:, g, 2 * HALF * h : 2 * HALF * (h + 1)].bitcast(FP4X4),
                        rhs_scale=w_scales[:, g, HALF * h : HALF * (h + 1)],
                        start=(s == 0),
                        stop=(s == PASSES - 1),
                    )
                x_psum[c, j, h] = acc

        def spread(c, rows_of_banks, name):
            wide = spread_pool.tile([P, D], BF16, name=name)
            for h in range(HALVES):
                cols = slice(HALF * h, HALF * (h + 1))
                nc.tensor.matmul(
                    out=wide[:, cols],
                    lhsT=ones[:],
                    rhs=rows_of_banks[:, cols],
                    start=True,
                    stop=True,
                )
            return wide

        def spread_gain(c):
            if exists(c) and first_tile_of(c) == 0:
                gain_psum[bank_of(c)] = spread(c, gain_row, "gain_wide")

        def spread_bias(c):
            if exists(c) and first_tile_of(c) == 0:
                bias_psum[bank_of(c)] = spread(c, bias_row, "bias_wide")

        def add_on_tensor(c, j, pool, tag):
            for h in range(HALVES):
                cols = slice(HALF * h, HALF * (h + 1))
                total = pool.tile([P, HALF], F32, name=tag)
                nc.tensor.matmul(
                    out=total[:],
                    lhsT=ident_bf16[:],
                    rhs=pw_tiles[c][:, j, cols],
                    start=True,
                    stop=False,
                )
                nc.tensor.matmul(
                    out=total[:],
                    lhsT=ones[:],
                    rhs=bias_row[:, cols],
                    start=False,
                    stop=True,
                )
                added[c, j, h] = total

        def copy_and_sum(c, j, h):
            if not exists(c):
                return
            if j == 0 and h == 0:
                y_tiles[c] = y_pool.tile([P, PAIR, D], F32, name="y_c")
                part_sum[c] = stats.tile([P, PAIR, HALVES], F32, name="sums")
            nc.scalar.activation(
                out=y_tiles[c][:, j, HALF * h : HALF * (h + 1)],
                in_=x_psum[c, j, h][:],
                func=ACT.Copy,
                accum_out=part_sum[c][:, j, h : h + 1],
            )

        def join_mean(c, j):
            if not exists(c):
                return
            if j == 0:
                scaled[c] = stats.tile([P, PAIR, HALVES], F32, name="scaled")
                negmean[c] = stats.tile([P, PAIR], F32, name="negmean")
            nc.scalar.activation(
                out=scaled[c][:, j, :],
                in_=part_sum[c][:, j, :],
                func=ACT.Copy,
                scale=-1.0 / D,
                accum_out=negmean[c][:, j : j + 1],
            )

        def sum_squares(c, j):
            if not exists(c):
                return
            if j == 0:
                sq[c] = stats.tile([P, PAIR], F32, name="sq")
            dropped = unread.tile([P, D], BF16)
            nc.scalar.activation(
                out=dropped[:],
                in_=y_tiles[c][:, j, :],
                func=ACT.Square,
                bias=negmean[c][:, j : j + 1],
                scale=1.0,
                accum_out=sq[c][:, j : j + 1],
            )

        def root(c, tiles):
            if not exists(c):
                return
            if tiles.start == 0:
                rstd[c] = stats.tile([P, PAIR], F32, name="rstd")
            nc.scalar.activation(
                out=rstd[c][:, tiles.start : tiles.stop],
                in_=sq[c][:, tiles.start : tiles.stop],
                func=ACT.Abs_reciprocal_sqrt,
                bias=eps[:, 0:1],
                scale=1.0 / D,
            )

        def centre_times_gain(c, j):
            if not exists(c):
                return
            if j == 0:
                o_tiles[c] = o_pool.tile([P, PAIR, D], F32, name="o_c")
            width = HALF if (c, j) in HALVED else D
            nc.vector.scalar_tensor_tensor(
                out=o_tiles[c][:, j, 0:width],
                in0=y_tiles[c][:, j, 0:width],
                scalar=negmean[c][:, j : j + 1],
                in1=gain_psum[bank_of(c)][:, 0:width],
                op0=ALU.add,
                op1=ALU.mult,
            )

        def copy_gain_for_gpsimd(n):
            nc.vector.tensor_copy(out=gain_sbuf[:, n, :], in_=gain_psum[n][:, HALF:])

        def centre_times_gain_on_gpsimd(c, j):
            centred = helper.tile([P, HALF], F32)
            nc.gpsimd.tensor_scalar(
                out=centred[:],
                in0=y_tiles[c][:, j, HALF:],
                scalar1=1.0,
                scalar2=negmean[c][:, j : j + 1],
                op0=ALU.mult,
                op1=ALU.add,
            )
            nc.gpsimd.tensor_tensor(
                out=o_tiles[c][:, j, HALF:],
                in0=centred[:],
                in1=gain_sbuf[:, bank_of(c), :],
                op=ALU.mult,
            )

        def finish(c, j):
            if not exists(c):
                return
            o_c = o_tiles[c]
            if (c, j, 0) in added:
                for h in range(HALVES):
                    cols = slice(HALF * h, HALF * (h + 1))
                    nc.vector.scalar_tensor_tensor(
                        out=o_c[:, j, cols],
                        in0=o_c[:, j, cols],
                        scalar=rstd[c][:, j : j + 1],
                        in1=added[c, j, h][:],
                        op0=ALU.mult,
                        op1=ALU.add,
                    )
                    nc.sync.dma_start(
                        out=out_rows[bank_of(c), :, first_tile_of(c) + j, cols], in_=o_c[:, j, cols]
                    )
                return
            nc.vector.scalar_tensor_tensor(
                out=o_c[:, j, :],
                in0=o_c[:, j, :],
                scalar=rstd[c][:, j : j + 1],
                in1=bias_psum[bank_of(c)][:],
                op0=ALU.mult,
                op1=ALU.add,
            )
            nc.gpsimd.tensor_tensor(
                out=o_c[:, j, :], in0=o_c[:, j, :], in1=pw_tiles[c][:, j, :], op=ALU.add
            )
            nc.sync.dma_start(
                out=out_rows[bank_of(c), :, first_tile_of(c) + j, :], in_=o_c[:, j, :]
            )

        def load_ahead(c):
            for j in range(PAIR):
                load_x(c + X_AHEAD, j)
            if exists(c + X_AHEAD) and first_tile_of(c + X_AHEAD) == 0:
                load_weight_scales(bank_of(c + X_AHEAD))
                for h in range(HALVES):
                    load_weight_words(bank_of(c + X_AHEAD), h)
            load_proto_w(c + PW_AHEAD)
            if c in (0, 5):
                load_gain(1 + (0, 5).index(c))
            if c in (2, 6):
                load_bias(1 + (2, 6).index(c))

        load_x(0, 0)
        load_weight_scales(0)
        load_gain(0)
        load_weight_words(0, 0)
        load_x(0, 1)
        load_weight_words(0, 1)
        load_bias(0)
        for c in (1, 2):
            for j in range(PAIR):
                load_x(c, j)
        load_proto_w(0)
        for j in range(PAIR):
            load_x(3, j)
        load_proto_w(1)

        warm_up(4)
        transpose(0, 0)
        spread_gain(0)
        regroup(0, 0, "scalar")
        quantise(0, range(0, 1))
        transpose(0, 1)
        regroup(0, 1, "scalar")
        quantise(0, range(1, 2))
        copy_gain_for_gpsimd(0)
        multiply(0, 0)
        transpose(1, 0)
        transpose(1, 1)
        multiply(0, 1)
        copy_and_sum(0, 0, 0)
        copy_and_sum(0, 0, 1)
        join_mean(0, 0)
        regroup(1, 0, "vector")
        regroup(1, 1, "vector")
        quantise(1, range(PAIR))
        nc.vector.memset(w_scales[:, PASSES:, :].bitcast(I32), 0)
        centre_times_gain(0, 0)
        centre_times_gain_on_gpsimd(0, 0)
        sum_squares(0, 0)
        transpose(2, 0)
        transpose(2, 1)
        copy_and_sum(0, 1, 0)
        copy_and_sum(0, 1, 1)
        multiply(1, 0)
        multiply(1, 1)
        join_mean(0, 1)
        spread_bias(0)
        regroup(2, 0, "vector")
        regroup(2, 1, "vector")
        centre_times_gain(0, 1)
        centre_times_gain_on_gpsimd(0, 1)
        sum_squares(0, 1)
        load_ahead(0)

        for c in range(1, CHUNKS + 1):
            load_ahead(c)
            if c < CHUNKS:
                root(c - 1, range(0, 1))
            if c > 1:
                spread_bias(c - 1)
            finish(c - 1, 0)
            quantise(c + 1, range(PAIR))
            spread_gain(c)
            for j in range(PAIR):
                transpose(c + 2, j)
            copy_and_sum(c, 0, 0)
            if c < CHUNKS:
                root(c - 1, range(1, 2))
            copy_and_sum(c, 0, 1)
            copy_and_sum(c, 1, 0)
            join_mean(c, 0)
            copy_and_sum(c, 1, 1)
            for j in range(PAIR):
                multiply(c + 1, j)
            if c == CHUNKS - 1:
                add_on_tensor(c - 1, 1, acc_pool, "acc")
                add_on_tensor(c, 0, xt_pool, "xt")
                add_on_tensor(c, 1, acc_pool, "acc")
            finish(c - 1, 1)
            if c == CHUNKS - 2:
                add_on_tensor(c, 0, xt_pool, "xt")
            regroup(c + 2, 0, "scalar")
            join_mean(c, 1)
            regroup(c + 2, 1, "vector" if c % 2 == 0 or c == CHUNKS - 3 else "scalar")
            if c == CHUNKS - 3:
                add_on_tensor(c, 1, xt_pool, "xt")
            for j in range(PAIR):
                centre_times_gain(c, j)
            if c == CHUNKS - 3:
                copy_gain_for_gpsimd(BANKS - 1)
            for j in range(PAIR):
                if (c, j) in HALVED:
                    centre_times_gain_on_gpsimd(c, j)
            for j in range(PAIR):
                sum_squares(c, j)
                if c == CHUNKS - 1:
                    root(c, range(j, j + 1))
